import numpy as np
import ml_dtypes


def mxq(x, axis, fmt="e4m3"):
    dtype, down = {"e4m3": (ml_dtypes.float8_e4m3fn, 7), "e5m2": (ml_dtypes.float8_e5m2, 14)}[fmt]
    v = np.moveaxis(np.asarray(x, np.float32).astype(ml_dtypes.bfloat16).astype(np.float64), axis, -1)
    blocks = v.reshape(v.shape[:-1] + (-1, 32))
    amax = np.abs(blocks).max(-1, keepdims=True)
    byte = np.maximum(np.where(amax > 0, np.frexp(amax)[1] - 1 + 127, 0) - down, 1)
    scale = np.exp2(byte - 127.0)
    codes = (blocks / scale).astype(np.float32).astype(dtype).astype(np.float64)
    return np.moveaxis((codes * scale).reshape(v.shape), -1, axis)


WIDE = False


def mx_kscale(k):
    if not WIDE:
        return np.ones(k)
    levels = np.array([10, -10, 5, -5, 0])
    a = np.random.permutation(np.resize(levels, k // 512 * 4)).reshape(k // 512, 4)
    idx = np.arange(k)
    return np.exp2(a[idx // 512, idx % 128 // 32])


BF16 = ml_dtypes.bfloat16


def bf(x):
    return np.asarray(x, np.float32).astype(BF16)


def f64(x):
    return np.asarray(x).astype(np.float64)


B, C, H, W, O = 4, 128, 128, 128, 128
K = 4 * C


def haar_dwt2(x):
    nb, nc_, nh, nw = x.shape
    xr = x.reshape(nb, nc_, nh // 2, 2, nw // 2, 2)
    a = xr[:, :, :, 0, :, 0]
    b = xr[:, :, :, 0, :, 1]
    c = xr[:, :, :, 1, :, 0]
    d = xr[:, :, :, 1, :, 1]
    half = 0.5
    LL = (a + b + c + d) * half
    LH = (a + b - c - d) * half
    HL = (a - b + c - d) * half
    HH = (a - b - c + d) * half
    return LL, LH, HL, HH


def setup_inputs():
    sc = mx_kscale(K)[::4]
    sk = np.repeat(sc, 4)
    return {"x": bf(np.random.standard_normal((B, C, H, W)) * sc[None, :, None, None]),
            "w_fusion": bf(np.random.standard_normal((O, K, 1, 1)) / np.sqrt(K) / sk[None, :, None, None])}


def reference(x, w_fusion):
    x = f64(x)
    nb, nc_, nh, nw = x.shape
    LL, LH, HL, HH = haar_dwt2(x)
    combined = np.stack([LL, LH, HL, HH], axis=2)
    combined = combined.reshape(nb, nc_ * 4, nh // 2, nw // 2)
    w = f64(w_fusion)[:, :, 0, 0]
    return np.einsum('bchw,oc->bohw', mxq(combined, 1, "e4m3"), mxq(w, 1, "e4m3"), optimize=True)

@@ -1,0 +1,131 @@
+from contextlib import ExitStack
+
+import concourse.mybir as mybir
+from concourse.masks import make_identity
+
+FP8X4 = mybir.dt.float8_e4m3fn_x4
+BF16 = mybir.dt.bfloat16
+F32 = mybir.dt.float32
+U32 = mybir.dt.uint32
+U8 = mybir.dt.uint8
+ADD = mybir.AluOpType.add
+SUB = mybir.AluOpType.subtract
+COPY = mybir.ActivationFunctionType.Copy
+
+P = 128
+B, C, H, W, O = 4, 128, 128, 128, 128
+PAIRS = 16
+ROWS = 2 * PAIRS
+NP = PAIRS * (W // 2)
+RUN = 4
+NG = NP // RUN
+N_TILE = 512
+CHUNKS_PER_IMAGE = H // ROWS
+NCH = B * CHUNKS_PER_IMAGE
+AHEAD = 3
+
+FLOPS = 2 * B * (H // 2) * (W // 2) * 4 * C * O
+
+
+def tile_haarwaveletlayer_kernel(tc, x, w_fusion, out):
+    nc = tc.nc
+    with ExitStack() as ctx:
+        const = ctx.enter_context(tc.tile_pool(name="const", bufs=1))
+        xin = ctx.enter_context(tc.tile_pool(name="xin", bufs=AHEAD + 1))
+        zpool = ctx.enter_context(tc.tile_pool(name="zpool", bufs=2))
+        gpool = ctx.enter_context(tc.tile_pool(name="gpool", bufs=2))
+        qpool = ctx.enter_context(tc.tile_pool(name="qpool", bufs=2))
+        opool = ctx.enter_context(tc.tile_pool(name="opool", bufs=3))
+        psw = ctx.enter_context(tc.psum_pool(name="psw", bufs=1))
+        psa = ctx.enter_context(tc.psum_pool(name="psa", bufs=4))
+        ctx.enter_context(tc.manual_schedule())
+
+        xt = {}
+        zt = {}
+        gt = {}
+
+        def load(k):
+            n, part = divmod(k, CHUNKS_PER_IMAGE)
+            x_sb = xin.tile([P, ROWS, W], BF16)
+            nc.sync.dma_start(out=x_sb[:], in_=x[n, :, part * ROWS : (part + 1) * ROWS, :])
+            xt[k] = x_sb
+
+        def vertical(k, v, op):
+            xv = xt[k][:].rearrange("p (i r) (g e q) -> p r q i g e", r=2, e=RUN, q=2)
+            zv = zt[k][:, :, 0:4, :].rearrange("p (i g) (q v) e -> p v q i g e", i=PAIRS, q=2)
+            nc.vector.tensor_tensor(out=zv[:, v], in0=xv[:, 0], in1=xv[:, 1], op=op)
+
+        def negate(k):
+            z_sb = zt[k]
+            nc.scalar.activation(out=z_sb[:, :, 4:6, :], in_=z_sb[:, :, 2:4, :], func=COPY, scale=-1.0)
+
+        def horizontal(k):
+            z_sb = zt[k]
+            g_sb = gpool.tile([P, 4 * NP], BF16, align_bytes=64)
+            gt[k] = g_sb
+            nc.vector.tensor_tensor(
+                out=g_sb[:].rearrange("p (g e s v) -> p g s v e", e=RUN, s=2, v=2),
+                in0=z_sb[:, :, 0:2, :].unsqueeze(2).to_broadcast([P, NG, 2, 2, RUN]),
+                in1=z_sb[:, :, 2:6, :].rearrange("p g (s v) e -> p g s v e", s=2),
+                op=ADD,
+            )
+
+        def finish(k):
+            n, part = divmod(k, CHUNKS_PER_IMAGE)
+            codes = qpool.tile([P, NP], U32, align_bytes=64)
+            scales = qpool.tile([P, NP], U8, align_bytes=64)
+            nc.vector.quantize_mx(out=codes[:].bitcast(FP8X4), scales=scales[:], in_=gt[k][:])
+            o_sb = opool.tile([P, NP], F32)
+            for h in range(NP // N_TILE):
+                cols = slice(h * N_TILE, (h + 1) * N_TILE)
+                acc = psa.tile([P, N_TILE], F32)
+                nc.tensor.matmul_mx(
+                    out=acc[:],
+                    lhsT=w_codes[:].bitcast(FP8X4),
+                    lhsT_scale=w_scales[:],
+                    rhs=codes[:, cols].bitcast(FP8X4),
+                    rhs_scale=scales[:, cols],
+                    start=True,
+                    stop=True,
+                )
+                nc.scalar.activation(out=o_sb[:, cols], in_=acc[:], func=COPY, scale=0.5)
+            nc.scalar.dma_start(
+                out=out[n, :, part * PAIRS : (part + 1) * PAIRS, :].rearrange("o i j -> o (i j)"),
+                in_=o_sb[:],
+            )
+
+        for k in range(AHEAD):
+            load(k)
+
+        w_sb = const.tile([P, 4 * C], BF16)
+        nc.scalar.dma_start(out=w_sb[:], in_=w_fusion.rearrange("o k a b -> o (k a b)"))
+        ident = const.tile([P, P], F32)
+        make_identity(nc, ident[:])
+        w_words = w_sb[:].bitcast(F32).rearrange("o (c u) -> o u c", u=2)
+        w_t = psw.tile([P, 2, O], F32)
+        for u in range(2):
+            nc.tensor.transpose(w_t[:, u, :], w_words[:, u, :], ident[:])
+        w_grouped = const.tile([P, 4 * O], BF16, align_bytes=64)
+        nc.scalar.copy(
+            out=w_grouped[:].bitcast(F32).rearrange("c (o u) -> c o u", u=2),
+            in_=w_t[:].rearrange("c u o -> c o u"),
+        )
+        w_codes = const.tile([P, O], U32, align_bytes=64)
+        w_scales = const.tile([P, O], U8, align_bytes=64)
+
+        for s in range(NCH + 2):
+            if s + AHEAD < NCH:
+                load(s + AHEAD)
+            if s == 1:
+                nc.vector.quantize_mx(out=w_codes[:].bitcast(FP8X4), scales=w_scales[:], in_=w_grouped[:])
+            if s < NCH:
+                z_sb = zpool.tile([P, NG, 6, RUN], F32)
+                zt[s] = z_sb
+                vertical(s, 0, ADD)
+            if s >= 2:
+                finish(s - 2)
+            if s < NCH:
+                vertical(s, 1, SUB)
+                negate(s)
+            if 1 <= s <= NCH:
+                horizontal(s - 1)

@@ -23,6 +23,11 @@ N_TILE = 512
 CHUNKS_PER_IMAGE = H // ROWS
 NCH = B * CHUNKS_PER_IMAGE
 AHEAD = 3
+QUADS = 4
+QPAIRS = PAIRS // QUADS
+QG = NG // QUADS
+NQ = NCH * QUADS
+G_GROUPS = 128
 
 FLOPS = 2 * B * (H // 2) * (W // 2) * 4 * C * O
 
@@ -32,15 +37,19 @@ def tile_haarwaveletlayer_kernel(tc, x, w_fusion, out):
     with ExitStack() as ctx:
         const = ctx.enter_context(tc.tile_pool(name="const", bufs=1))
         xin = ctx.enter_context(tc.tile_pool(name="xin", bufs=AHEAD + 1))
+        spool = ctx.enter_context(tc.tile_pool(name="spool", bufs=3))
         zpool = ctx.enter_context(tc.tile_pool(name="zpool", bufs=2))
         gpool = ctx.enter_context(tc.tile_pool(name="gpool", bufs=2))
         qpool = ctx.enter_context(tc.tile_pool(name="qpool", bufs=2))
         opool = ctx.enter_context(tc.tile_pool(name="opool", bufs=3))
-        psw = ctx.enter_context(tc.psum_pool(name="psw", bufs=1))
-        psa = ctx.enter_context(tc.psum_pool(name="psa", bufs=4))
+        psa = ctx.enter_context(tc.psum_pool(name="psa", bufs=2))
+        psb = ctx.enter_context(tc.psum_pool(name="psb", bufs=4))
+        psm = ctx.enter_context(tc.psum_pool(name="psm", bufs=2))
         ctx.enter_context(tc.manual_schedule())
 
         xt = {}
+        st = {}
+        bt = {}
         zt = {}
         gt = {}
 
@@ -50,23 +59,48 @@ def tile_haarwaveletlayer_kernel(tc, x, w_fusion, out):
             nc.sync.dma_start(out=x_sb[:], in_=x[n, :, part * ROWS : (part + 1) * ROWS, :])
             xt[k] = x_sb
 
-        def vertical(k, v, op):
+        def flip(t):
+            k, q = divmod(t, QUADS)
+            words = xt[k][:].rearrange("p r w -> p (r w)").bitcast(F32)
+            a_ps = psa.tile([P, 4 * P], F32)
+            for b in range(4):
+                nc.tensor.transpose(
+                    a_ps[:, b * P : (b + 1) * P], words[:, (4 * q + b) * P : (4 * q + b + 1) * P], ident[:]
+                )
+            s_sb = spool.tile([P, 4 * P], F32)
+            st[t] = s_sb
+            nc.scalar.copy(out=s_sb[:], in_=a_ps[:])
+
+        def flip_back(t):
+            b_ps = psb.tile([P, 4 * P], F32)
+            bt[t] = b_ps
+            for b in range(4):
+                nc.tensor.transpose(b_ps[:, b * P : (b + 1) * P], st[t][:, b * P : (b + 1) * P], ident[:])
+
+        def vertical_chunk(k, v, op):
             xv = xt[k][:].rearrange("p (i r) (g e q) -> p r q i g e", r=2, e=RUN, q=2)
             zv = zt[k][:, :, 0:4, :].rearrange("p (i g) (q v) e -> p v q i g e", i=PAIRS, q=2)
             nc.vector.tensor_tensor(out=zv[:, v], in0=xv[:, 0], in1=xv[:, 1], op=op)
+
+        def vertical_quad(t, v, op):
+            k, q = divmod(t, QUADS)
+            top = bt[t][:].bitcast(BF16).rearrange("p (i r g e q) -> p r q i g e", i=QPAIRS, r=2, e=RUN, q=2)
+            rows = xt[k][:, 2 * QPAIRS * q : 2 * QPAIRS * (q + 1), :]
+            bottom = rows.rearrange("p (i r) (g e q) -> p r q i g e", r=2, e=RUN, q=2)
+            zq = zt[k][:, QG * q : QG * (q + 1), 0:4, :]
+            zv = zq.rearrange("p (i g) (q v) e -> p v q i g e", i=QPAIRS, q=2)
+            nc.vector.tensor_tensor(out=zv[:, v], in0=top[:, 0], in1=bottom[:, 1], op=op)
 
         def negate(k):
             z_sb = zt[k]
             nc.scalar.activation(out=z_sb[:, :, 4:6, :], in_=z_sb[:, :, 2:4, :], func=COPY, scale=-1.0)
 
-        def horizontal(k):
+        def horizontal(engine, k, g0, g1):
             z_sb = zt[k]
-            g_sb = gpool.tile([P, 4 * NP], BF16, align_bytes=64)
-            gt[k] = g_sb
-            nc.vector.tensor_tensor(
-                out=g_sb[:].rearrange("p (g e s v) -> p g s v e", e=RUN, s=2, v=2),
-                in0=z_sb[:, :, 0:2, :].unsqueeze(2).to_broadcast([P, NG, 2, 2, RUN]),
-                in1=z_sb[:, :, 2:6, :].rearrange("p g (s v) e -> p g s v e", s=2),
+            engine.tensor_tensor(
+                out=gt[k][:, 16 * g0 : 16 * g1].rearrange("p (g e s v) -> p g s v e", e=RUN, s=2, v=2),
+                in0=z_sb[:, g0:g1, 0:2, :].unsqueeze(2).to_broadcast([P, g1 - g0, 2, 2, RUN]),
+                in1=z_sb[:, g0:g1, 2:6, :].rearrange("p g (s v) e -> p g s v e", s=2),
                 op=ADD,
             )
 
@@ -78,7 +112,7 @@ def tile_haarwaveletlayer_kernel(tc, x, w_fusion, out):
             o_sb = opool.tile([P, NP], F32)
             for h in range(NP // N_TILE):
                 cols = slice(h * N_TILE, (h + 1) * N_TILE)
-                acc = psa.tile([P, N_TILE], F32)
+                acc = psm.tile([P, N_TILE], F32)
                 nc.tensor.matmul_mx(
                     out=acc[:],
                     lhsT=w_codes[:].bitcast(FP8X4),
@@ -102,30 +136,46 @@ def tile_haarwaveletlayer_kernel(tc, x, w_fusion, out):
         ident = const.tile([P, P], F32)
         make_identity(nc, ident[:])
         w_words = w_sb[:].bitcast(F32).rearrange("o (c u) -> o u c", u=2)
-        w_t = psw.tile([P, 2, O], F32)
+        a_ps = psa.tile([P, 4 * P], F32)
         for u in range(2):
-            nc.tensor.transpose(w_t[:, u, :], w_words[:, u, :], ident[:])
+            nc.tensor.transpose(a_ps[:, u * O : (u + 1) * O], w_words[:, u, :], ident[:])
         w_grouped = const.tile([P, 4 * O], BF16, align_bytes=64)
         nc.scalar.copy(
             out=w_grouped[:].bitcast(F32).rearrange("c (o u) -> c o u", u=2),
-            in_=w_t[:].rearrange("c u o -> c o u"),
+            in_=a_ps[:, 0 : 2 * O].rearrange("c (u o) -> c o u", u=2),
         )
         w_codes = const.tile([P, O], U32, align_bytes=64)
         w_scales = const.tile([P, O], U8, align_bytes=64)
 
-        for s in range(NCH + 2):
-            if s + AHEAD < NCH:
-                load(s + AHEAD)
-            if s == 1:
-                nc.vector.quantize_mx(out=w_codes[:].bitcast(FP8X4), scales=w_scales[:], in_=w_grouped[:])
-            if s < NCH:
+        for t in range(NQ):
+            k, q = divmod(t, QUADS)
+            if q == 0:
+                if k + AHEAD < NCH:
+                    load(k + AHEAD)
                 z_sb = zpool.tile([P, NG, 6, RUN], F32)
-                zt[s] = z_sb
-                vertical(s, 0, ADD)
-            if s >= 2:
-                finish(s - 2)
-            if s < NCH:
-                vertical(s, 1, SUB)
-                negate(s)
-            if 1 <= s <= NCH:
-                horizontal(s - 1)
+                zt[k] = z_sb
+            if QUADS <= t + 4 < NQ:
+                flip(t + 4)
+            if QUADS <= t + 3 < NQ:
+                flip_back(t + 3)
+            if k == 0:
+                if q == 0:
+                    vertical_chunk(0, 0, ADD)
+                    vertical_chunk(0, 1, SUB)
+                    nc.vector.quantize_mx(out=w_codes[:].bitcast(FP8X4), scales=w_scales[:], in_=w_grouped[:])
+            else:
+                vertical_quad(t, 0, ADD)
+                vertical_quad(t, 1, SUB)
+            if q == QUADS - 1:
+                negate(k)
+                if k >= 1:
+                    horizontal(nc.vector, k - 1, 0, NG - G_GROUPS)
+                if k >= 2:
+                    finish(k - 2)
+                g_sb = gpool.tile([P, 4 * NP], BF16, align_bytes=64)
+                gt[k] = g_sb
+                if k < NCH - 1:
+                    horizontal(nc.gpsimd, k, NG - G_GROUPS, NG)
+        finish(NCH - 2)
+        horizontal(nc.vector, NCH - 1, 0, NG)
+        finish(NCH - 1)

@@ -23,10 +23,8 @@ N_TILE = 512
 CHUNKS_PER_IMAGE = H // ROWS
 NCH = B * CHUNKS_PER_IMAGE
 AHEAD = 3
-QUADS = 4
-QPAIRS = PAIRS // QUADS
-QG = NG // QUADS
-NQ = NCH * QUADS
+HPAIRS = PAIRS // 2
+HG = NG // 2
 G_GROUPS = 128
 
 FLOPS = 2 * B * (H // 2) * (W // 2) * 4 * C * O
@@ -37,7 +35,7 @@ def tile_haarwaveletlayer_kernel(tc, x, w_fusion, out):
     with ExitStack() as ctx:
         const = ctx.enter_context(tc.tile_pool(name="const", bufs=1))
         xin = ctx.enter_context(tc.tile_pool(name="xin", bufs=AHEAD + 1))
-        spool = ctx.enter_context(tc.tile_pool(name="spool", bufs=3))
+        spool = ctx.enter_context(tc.tile_pool(name="spool", bufs=4))
         zpool = ctx.enter_context(tc.tile_pool(name="zpool", bufs=2))
         gpool = ctx.enter_context(tc.tile_pool(name="gpool", bufs=2))
         qpool = ctx.enter_context(tc.tile_pool(name="qpool", bufs=2))
@@ -52,6 +50,8 @@ def tile_haarwaveletlayer_kernel(tc, x, w_fusion, out):
         bt = {}
         zt = {}
         gt = {}
+        qt = {}
+        ot = {}
 
         def load(k):
             n, part = divmod(k, CHUNKS_PER_IMAGE)
@@ -59,41 +59,40 @@ def tile_haarwaveletlayer_kernel(tc, x, w_fusion, out):
             nc.sync.dma_start(out=x_sb[:], in_=x[n, :, part * ROWS : (part + 1) * ROWS, :])
             xt[k] = x_sb
 
-        def flip(t):
-            k, q = divmod(t, QUADS)
-            words = xt[k][:].rearrange("p r w -> p (r w)").bitcast(F32)
-            a_ps = psa.tile([P, 4 * P], F32)
-            for b in range(4):
+        def flip(h):
+            k, half = divmod(h, 2)
+            a_ps = psa.tile([P, HPAIRS * P], BF16)
+            for j in range(HPAIRS):
                 nc.tensor.transpose(
-                    a_ps[:, b * P : (b + 1) * P], words[:, (4 * q + b) * P : (4 * q + b + 1) * P], ident[:]
+                    a_ps[:, j * P : (j + 1) * P], xt[k][:, 2 * (HPAIRS * half + j), :], ident_bf[:]
                 )
-            s_sb = spool.tile([P, 4 * P], F32)
-            st[t] = s_sb
+            s_sb = spool.tile([P, HPAIRS * P], BF16)
+            st[h] = s_sb
             nc.scalar.copy(out=s_sb[:], in_=a_ps[:])
 
-        def flip_back(t):
-            b_ps = psb.tile([P, 4 * P], F32)
-            bt[t] = b_ps
-            for b in range(4):
-                nc.tensor.transpose(b_ps[:, b * P : (b + 1) * P], st[t][:, b * P : (b + 1) * P], ident[:])
+        def flip_back(h):
+            b_ps = psb.tile([P, HPAIRS * P], BF16)
+            bt[h] = b_ps
+            for j in range(HPAIRS):
+                nc.tensor.transpose(b_ps[:, j * P : (j + 1) * P], st[h][:, j * P : (j + 1) * P], ident_bf[:])
 
         def vertical_chunk(k, v, op):
             xv = xt[k][:].rearrange("p (i r) (g e q) -> p r q i g e", r=2, e=RUN, q=2)
             zv = zt[k][:, :, 0:4, :].rearrange("p (i g) (q v) e -> p v q i g e", i=PAIRS, q=2)
             nc.vector.tensor_tensor(out=zv[:, v], in0=xv[:, 0], in1=xv[:, 1], op=op)
 
-        def vertical_quad(t, v, op):
-            k, q = divmod(t, QUADS)
-            top = bt[t][:].bitcast(BF16).rearrange("p (i r g e q) -> p r q i g e", i=QPAIRS, r=2, e=RUN, q=2)
-            rows = xt[k][:, 2 * QPAIRS * q : 2 * QPAIRS * (q + 1), :]
+        def vertical_half(h, v, op):
+            k, half = divmod(h, 2)
+            top = bt[h][:].rearrange("p (i g e q) -> p q i g e", i=HPAIRS, e=RUN, q=2)
+            rows = xt[k][:, 2 * HPAIRS * half : 2 * HPAIRS * (half + 1), :]
             bottom = rows.rearrange("p (i r) (g e q) -> p r q i g e", r=2, e=RUN, q=2)
-            zq = zt[k][:, QG * q : QG * (q + 1), 0:4, :]
-            zv = zq.rearrange("p (i g) (q v) e -> p v q i g e", i=QPAIRS, q=2)
-            nc.vector.tensor_tensor(out=zv[:, v], in0=top[:, 0], in1=bottom[:, 1], op=op)
+            zh = zt[k][:, HG * half : HG * (half + 1), 0:4, :]
+            zv = zh.rearrange("p (i g) (q v) e -> p v q i g e", i=HPAIRS, q=2)
+            nc.vector.tensor_tensor(out=zv[:, v], in0=top, in1=bottom[:, 1], op=op)
 
-        def negate(k):
+        def negate(k, g0, g1):
             z_sb = zt[k]
-            nc.scalar.activation(out=z_sb[:, :, 4:6, :], in_=z_sb[:, :, 2:4, :], func=COPY, scale=-1.0)
+            nc.scalar.activation(out=z_sb[:, g0:g1, 4:6, :], in_=z_sb[:, g0:g1, 2:4, :], func=COPY, scale=-1.0)
 
         def horizontal(engine, k, g0, g1):
             z_sb = zt[k]
@@ -104,29 +103,44 @@ def tile_haarwaveletlayer_kernel(tc, x, w_fusion, out):
                 op=ADD,
             )
 
-        def finish(k):
-            n, part = divmod(k, CHUNKS_PER_IMAGE)
-            codes = qpool.tile([P, NP], U32, align_bytes=64)
-            scales = qpool.tile([P, NP], U8, align_bytes=64)
-            nc.vector.quantize_mx(out=codes[:].bitcast(FP8X4), scales=scales[:], in_=gt[k][:])
-            o_sb = opool.tile([P, NP], F32)
-            for h in range(NP // N_TILE):
-                cols = slice(h * N_TILE, (h + 1) * N_TILE)
-                acc = psm.tile([P, N_TILE], F32)
-                nc.tensor.matmul_mx(
-                    out=acc[:],
-                    lhsT=w_codes[:].bitcast(FP8X4),
-                    lhsT_scale=w_scales[:],
-                    rhs=codes[:, cols].bitcast(FP8X4),
-                    rhs_scale=scales[:, cols],
-                    start=True,
-                    stop=True,
-                )
-                nc.scalar.activation(out=o_sb[:, cols], in_=acc[:], func=COPY, scale=0.5)
-            nc.scalar.dma_start(
-                out=out[n, :, part * PAIRS : (part + 1) * PAIRS, :].rearrange("o i j -> o (i j)"),
-                in_=o_sb[:],
+        def quantise(k, c0, c1):
+            if c0 == 0:
+                codes = qpool.tile([P, NP], U32, align_bytes=64)
+                scales = qpool.tile([P, NP], U8, align_bytes=64)
+                qt[k] = (codes, scales)
+            codes, scales = qt[k]
+            nc.vector.quantize_mx(
+                out=codes[:, c0:c1].bitcast(FP8X4), scales=scales[:, c0:c1], in_=gt[k][:, 4 * c0 : 4 * c1]
             )
+
+        def multiply(k, h):
+            codes, scales = qt[k]
+            if h == 0:
+                o_sb = opool.tile([P, NP], F32)
+                ot[k] = o_sb
+            cols = slice(h * N_TILE, (h + 1) * N_TILE)
+            acc = psm.tile([P, N_TILE], F32)
+            nc.tensor.matmul_mx(
+                out=acc[:],
+                lhsT=w_codes[:].bitcast(FP8X4),
+                lhsT_scale=w_scales[:],
+                rhs=codes[:, cols].bitcast(FP8X4),
+                rhs_scale=scales[:, cols],
+                start=True,
+                stop=True,
+            )
+            nc.scalar.activation(out=ot[k][:, cols], in_=acc[:], func=COPY, scale=0.5)
+
+        def store(k, c0, c1):
+            n, part = divmod(k, CHUNKS_PER_IMAGE)
+            i0 = part * PAIRS + c0 // (W // 2)
+            i1 = part * PAIRS + c1 // (W // 2)
+            nc.scalar.dma_start(out=out[n, :, i0:i1, :].rearrange("o i j -> o (i j)"), in_=ot[k][:, c0:c1])
+
+        def emit(k):
+            multiply(k, 0)
+            multiply(k, 1)
+            store(k, 0, NP)
 
         for k in range(AHEAD):
             load(k)
@@ -135,6 +149,8 @@ def tile_haarwaveletlayer_kernel(tc, x, w_fusion, out):
         nc.scalar.dma_start(out=w_sb[:], in_=w_fusion.rearrange("o k a b -> o (k a b)"))
         ident = const.tile([P, P], F32)
         make_identity(nc, ident[:])
+        ident_bf = const.tile([P, P], BF16)
+        make_identity(nc, ident_bf[:])
         w_words = w_sb[:].bitcast(F32).rearrange("o (c u) -> o u c", u=2)
         a_ps = psa.tile([P, 4 * P], F32)
         for u in range(2):
@@ -146,36 +162,48 @@ def tile_haarwaveletlayer_kernel(tc, x, w_fusion, out):
         )
         w_codes = const.tile([P, O], U32, align_bytes=64)
         w_scales = const.tile([P, O], U8, align_bytes=64)
+        flip(2)
+        flip(3)
 
-        for t in range(NQ):
-            k, q = divmod(t, QUADS)
-            if q == 0:
-                if k + AHEAD < NCH:
-                    load(k + AHEAD)
-                z_sb = zpool.tile([P, NG, 6, RUN], F32)
-                zt[k] = z_sb
-            if QUADS <= t + 4 < NQ:
-                flip(t + 4)
-            if QUADS <= t + 3 < NQ:
-                flip_back(t + 3)
+        for k in range(NCH):
+            if k + AHEAD < NCH:
+                load(k + AHEAD)
+            if k >= 3:
+                emit(k - 3)
+            if k + 1 < NCH:
+                flip_back(2 * k + 2)
+                flip_back(2 * k + 3)
+            if k + 2 < NCH:
+                flip(2 * k + 4)
+                flip(2 * k + 5)
+            z_sb = zpool.tile([P, NG, 6, RUN], F32)
+            zt[k] = z_sb
             if k == 0:
-                if q == 0:
-                    vertical_chunk(0, 0, ADD)
-                    vertical_chunk(0, 1, SUB)
-                    nc.vector.quantize_mx(out=w_codes[:].bitcast(FP8X4), scales=w_scales[:], in_=w_grouped[:])
+                vertical_chunk(0, 0, ADD)
+                vertical_chunk(0, 1, SUB)
+                negate(0, 0, NG)
+                nc.vector.quantize_mx(out=w_codes[:].bitcast(FP8X4), scales=w_scales[:], in_=w_grouped[:])
             else:
-                vertical_quad(t, 0, ADD)
-                vertical_quad(t, 1, SUB)
-            if q == QUADS - 1:
-                negate(k)
-                if k >= 1:
-                    horizontal(nc.vector, k - 1, 0, NG - G_GROUPS)
-                if k >= 2:
-                    finish(k - 2)
-                g_sb = gpool.tile([P, 4 * NP], BF16, align_bytes=64)
-                gt[k] = g_sb
-                if k < NCH - 1:
-                    horizontal(nc.gpsimd, k, NG - G_GROUPS, NG)
-        finish(NCH - 2)
-        horizontal(nc.vector, NCH - 1, 0, NG)
-        finish(NCH - 1)
+                for half in range(2):
+                    vertical_half(2 * k + half, 0, ADD)
+                    vertical_half(2 * k + half, 1, SUB)
+                    negate(k, HG * half, HG * (half + 1))
+            if k >= 1:
+                horizontal(nc.vector, k - 1, 0, NG - G_GROUPS)
+            if k >= 2:
+                quantise(k - 2, 0, NP)
+            g_sb = gpool.tile([P, 4 * NP], BF16, align_bytes=64)
+            gt[k] = g_sb
+            if k < NCH - 1:
+                horizontal(nc.gpsimd, k, NG - G_GROUPS, NG)
+
+        last = NCH - 1
+        emit(last - 2)
+        quantise(last - 1, 0, NP)
+        emit(last - 1)
+        horizontal(nc.vector, last, 0, HG)
+        horizontal(nc.vector, last, HG, NG)
+        for h in range(2):
+            quantise(last, h * N_TILE, (h + 1) * N_TILE)
+            multiply(last, h)
+            store(last, h * N_TILE, (h + 1) * N_TILE)

@@ -25,7 +25,7 @@ NCH = B * CHUNKS_PER_IMAGE
 AHEAD = 3
 HPAIRS = PAIRS // 2
 HG = NG // 2
-G_GROUPS = 128
+G_GROUPS = 112
 
 FLOPS = 2 * B * (H // 2) * (W // 2) * 4 * C * O
 
@@ -46,6 +46,7 @@ def tile_haarwaveletlayer_kernel(tc, x, w_fusion, out):
         ctx.enter_context(tc.manual_schedule())
 
         xt = {}
+        at = {}
         st = {}
         bt = {}
         zt = {}
@@ -66,9 +67,12 @@ def tile_haarwaveletlayer_kernel(tc, x, w_fusion, out):
                 nc.tensor.transpose(
                     a_ps[:, j * P : (j + 1) * P], xt[k][:, 2 * (HPAIRS * half + j), :], ident_bf[:]
                 )
+            at[h] = a_ps
+
+        def flip_copy(h):
             s_sb = spool.tile([P, HPAIRS * P], BF16)
             st[h] = s_sb
-            nc.scalar.copy(out=s_sb[:], in_=a_ps[:])
+            nc.scalar.copy(out=s_sb[:], in_=at[h][:])
 
         def flip_back(h):
             b_ps = psb.tile([P, HPAIRS * P], BF16)
@@ -164,6 +168,8 @@ def tile_haarwaveletlayer_kernel(tc, x, w_fusion, out):
         w_scales = const.tile([P, O], U8, align_bytes=64)
         flip(2)
         flip(3)
+        flip_copy(2)
+        flip_copy(3)
 
         for k in range(NCH):
             if k + AHEAD < NCH:
@@ -188,6 +194,9 @@ def tile_haarwaveletlayer_kernel(tc, x, w_fusion, out):
                     vertical_half(2 * k + half, 0, ADD)
                     vertical_half(2 * k + half, 1, SUB)
                     negate(k, HG * half, HG * (half + 1))
+            if k + 2 < NCH:
+                flip_copy(2 * k + 4)
+                flip_copy(2 * k + 5)
             if k >= 1:
                 horizontal(nc.vector, k - 1, 0, NG - G_GROUPS)
             if k >= 2:

@@ -20,12 +20,15 @@ NP = PAIRS * (W // 2)
 RUN = 4
 NG = NP // RUN
 N_TILE = 512
+BANK = 512
 CHUNKS_PER_IMAGE = H // ROWS
 NCH = B * CHUNKS_PER_IMAGE
 AHEAD = 3
 HPAIRS = PAIRS // 2
 HG = NG // 2
-G_GROUPS = 112
+BANK_G = BANK // (2 * RUN)
+V_GROUPS = 104
+HEAD_PIECES = 4
 
 FLOPS = 2 * B * (H // 2) * (W // 2) * 4 * C * O
 
@@ -35,7 +38,8 @@ def tile_haarwaveletlayer_kernel(tc, x, w_fusion, out):
     with ExitStack() as ctx:
         const = ctx.enter_context(tc.tile_pool(name="const", bufs=1))
         xin = ctx.enter_context(tc.tile_pool(name="xin", bufs=AHEAD + 1))
-        spool = ctx.enter_context(tc.tile_pool(name="spool", bufs=4))
+        spool_x = ctx.enter_context(tc.tile_pool(name="spool_x", bufs=4))
+        spool_e = ctx.enter_context(tc.tile_pool(name="spool_e", bufs=2))
         zpool = ctx.enter_context(tc.tile_pool(name="zpool", bufs=2))
         gpool = ctx.enter_context(tc.tile_pool(name="gpool", bufs=2))
         qpool = ctx.enter_context(tc.tile_pool(name="qpool", bufs=2))
@@ -45,7 +49,8 @@ def tile_haarwaveletlayer_kernel(tc, x, w_fusion, out):
         psm = ctx.enter_context(tc.psum_pool(name="psm", bufs=2))
         ctx.enter_context(tc.manual_schedule())
 
-        xt = {}
+        xe = {}
+        xo = {}
         at = {}
         st = {}
         bt = {}
@@ -56,56 +61,75 @@ def tile_haarwaveletlayer_kernel(tc, x, w_fusion, out):
 
         def load(k):
             n, part = divmod(k, CHUNKS_PER_IMAGE)
-            x_sb = xin.tile([P, ROWS, W], BF16)
-            nc.sync.dma_start(out=x_sb[:], in_=x[n, :, part * ROWS : (part + 1) * ROWS, :])
-            xt[k] = x_sb
+            rows = x[n, :, part * ROWS : (part + 1) * ROWS, :].rearrange("c (i r) w -> c r i w", r=2)
+            x_even = xin.tile([P, PAIRS, W], BF16)
+            nc.sync.dma_start(out=x_even[:], in_=rows[:, 0])
+            xe[k] = x_even
+            x_odd = xin.tile([P, PAIRS, W], BF16)
+            nc.sync.dma_start(out=x_odd[:], in_=rows[:, 1])
+            xo[k] = x_odd
 
-        def flip(h):
-            k, half = divmod(h, 2)
-            a_ps = psa.tile([P, HPAIRS * P], BF16)
-            for j in range(HPAIRS):
-                nc.tensor.transpose(
-                    a_ps[:, j * P : (j + 1) * P], xt[k][:, 2 * (HPAIRS * half + j), :], ident_bf[:]
-                )
-            at[h] = a_ps
+        def flip(key, source, blocks):
+            a_ps = psa.tile([P, BANK], F32)
+            for b in range(blocks):
+                nc.tensor.transpose(a_ps[:, b * P : (b + 1) * P], source[:, b * P : (b + 1) * P], ident[:])
+            at[key] = a_ps
 
-        def flip_copy(h):
-            s_sb = spool.tile([P, HPAIRS * P], BF16)
-            st[h] = s_sb
-            nc.scalar.copy(out=s_sb[:], in_=at[h][:])
+        def flip_copy(pool, key, blocks):
+            s_sb = pool.tile([P, BANK], F32)
+            st[key] = s_sb
+            nc.scalar.copy(out=s_sb[:, 0 : blocks * P], in_=at[key][:, 0 : blocks * P])
 
-        def flip_back(h):
-            b_ps = psb.tile([P, HPAIRS * P], BF16)
-            bt[h] = b_ps
-            for j in range(HPAIRS):
-                nc.tensor.transpose(b_ps[:, j * P : (j + 1) * P], st[h][:, j * P : (j + 1) * P], ident_bf[:])
+        def flip_back(key, blocks):
+            b_ps = psb.tile([P, BANK], F32)
+            bt[key] = b_ps
+            for b in range(blocks):
+                nc.tensor.transpose(b_ps[:, b * P : (b + 1) * P], st[key][:, b * P : (b + 1) * P], ident[:])
 
-        def vertical_chunk(k, v, op):
-            xv = xt[k][:].rearrange("p (i r) (g e q) -> p r q i g e", r=2, e=RUN, q=2)
-            zv = zt[k][:, :, 0:4, :].rearrange("p (i g) (q v) e -> p v q i g e", i=PAIRS, q=2)
-            nc.vector.tensor_tensor(out=zv[:, v], in0=xv[:, 0], in1=xv[:, 1], op=op)
+        def even_rows(k, half):
+            return xe[k][:].rearrange("p i w -> p (i w)").bitcast(F32)[:, half * BANK : (half + 1) * BANK]
 
-        def vertical_half(h, v, op):
-            k, half = divmod(h, 2)
-            top = bt[h][:].rearrange("p (i g e q) -> p q i g e", i=HPAIRS, e=RUN, q=2)
-            rows = xt[k][:, 2 * HPAIRS * half : 2 * HPAIRS * (half + 1), :]
-            bottom = rows.rearrange("p (i r) (g e q) -> p r q i g e", r=2, e=RUN, q=2)
-            zh = zt[k][:, HG * half : HG * (half + 1), 0:4, :]
-            zv = zh.rearrange("p (i g) (q v) e -> p v q i g e", i=HPAIRS, q=2)
-            nc.vector.tensor_tensor(out=zv[:, v], in0=top, in1=bottom[:, 1], op=op)
+        def even_columns(k, part):
+            return zt[k][:, 0].rearrange("p g v e -> p (g v e)")[:, part * BANK : (part + 1) * BANK]
+
+        def e_blocks(part):
+            groups = min(V_GROUPS - part * BANK_G, BANK_G)
+            return (groups * 2 * RUN + P - 1) // P
+
+        def vertical(k, top, bottom, g0, pairs, v, op):
+            zv = zt[k][:, 0:2, g0 : g0 + pairs * (NG // PAIRS)].rearrange("p q (i g) v e -> p v q i g e", i=pairs)
+            nc.vector.tensor_tensor(
+                out=zv[:, v],
+                in0=top.rearrange("p i (g e q) -> p q i g e", e=RUN, q=2),
+                in1=bottom.rearrange("p i (g e q) -> p q i g e", e=RUN, q=2),
+                op=op,
+            )
+
+        def vertical_half(k, half):
+            top = bt["x", k, half][:].bitcast(BF16).rearrange("p (i w) -> p i w", i=HPAIRS)
+            bottom = xo[k][:, half * HPAIRS : (half + 1) * HPAIRS, :]
+            vertical(k, top, bottom, half * HG, HPAIRS, 0, ADD)
+            vertical(k, top, bottom, half * HG, HPAIRS, 1, SUB)
 
         def negate(k, g0, g1):
-            z_sb = zt[k]
-            nc.scalar.activation(out=z_sb[:, g0:g1, 4:6, :], in_=z_sb[:, g0:g1, 2:4, :], func=COPY, scale=-1.0)
+            nc.scalar.activation(out=zt[k][:, 2, g0:g1], in_=zt[k][:, 1, g0:g1], func=COPY, scale=-1.0)
 
-        def horizontal(engine, k, g0, g1):
-            z_sb = zt[k]
+        def horizontal(engine, k, g0, g1, even):
             engine.tensor_tensor(
                 out=gt[k][:, 16 * g0 : 16 * g1].rearrange("p (g e s v) -> p g s v e", e=RUN, s=2, v=2),
-                in0=z_sb[:, g0:g1, 0:2, :].unsqueeze(2).to_broadcast([P, g1 - g0, 2, 2, RUN]),
-                in1=z_sb[:, g0:g1, 2:6, :].rearrange("p g (s v) e -> p g s v e", s=2),
+                in0=even.unsqueeze(2).to_broadcast([P, g1 - g0, 2, 2, RUN]),
+                in1=zt[k][:, 1:3, g0:g1].rearrange("p s g v e -> p g s v e"),
                 op=ADD,
             )
+
+        def horizontal_sbuf(engine, k, g0, g1):
+            horizontal(engine, k, g0, g1, zt[k][:, 0, g0:g1])
+
+        def horizontal_psum(k, part):
+            g0 = part * BANK_G
+            g1 = min(V_GROUPS, g0 + BANK_G)
+            even = bt["e", k, part][:, 0 : (g1 - g0) * 2 * RUN].rearrange("p (g v e) -> p g v e", v=2, e=RUN)
+            horizontal(nc.vector, k, g0, g1, even)
 
         def quantise(k, c0, c1):
             if c0 == 0:
@@ -117,23 +141,22 @@ def tile_haarwaveletlayer_kernel(tc, x, w_fusion, out):
                 out=codes[:, c0:c1].bitcast(FP8X4), scales=scales[:, c0:c1], in_=gt[k][:, 4 * c0 : 4 * c1]
             )
 
-        def multiply(k, h):
+        def multiply(k, c0, c1):
             codes, scales = qt[k]
-            if h == 0:
+            if c0 == 0:
                 o_sb = opool.tile([P, NP], F32)
                 ot[k] = o_sb
-            cols = slice(h * N_TILE, (h + 1) * N_TILE)
             acc = psm.tile([P, N_TILE], F32)
             nc.tensor.matmul_mx(
-                out=acc[:],
+                out=acc[:, 0 : c1 - c0],
                 lhsT=w_codes[:].bitcast(FP8X4),
                 lhsT_scale=w_scales[:],
-                rhs=codes[:, cols].bitcast(FP8X4),
-                rhs_scale=scales[:, cols],
+                rhs=codes[:, c0:c1].bitcast(FP8X4),
+                rhs_scale=scales[:, c0:c1],
                 start=True,
                 stop=True,
             )
-            nc.scalar.activation(out=ot[k][:, cols], in_=acc[:], func=COPY, scale=0.5)
+            nc.scalar.activation(out=ot[k][:, c0:c1], in_=acc[:, 0 : c1 - c0], func=COPY, scale=0.5)
 
         def store(k, c0, c1):
             n, part = divmod(k, CHUNKS_PER_IMAGE)
@@ -142,21 +165,26 @@ def tile_haarwaveletlayer_kernel(tc, x, w_fusion, out):
             nc.scalar.dma_start(out=out[n, :, i0:i1, :].rearrange("o i j -> o (i j)"), in_=ot[k][:, c0:c1])
 
         def emit(k):
-            multiply(k, 0)
-            multiply(k, 1)
+            multiply(k, 0, N_TILE)
+            multiply(k, N_TILE, NP)
             store(k, 0, NP)
 
-        for k in range(AHEAD):
+        x_first = const.tile([P, ROWS, W], BF16)
+        piece_rows = ROWS // HEAD_PIECES
+        for i in range(HEAD_PIECES):
+            nc.sync.dma_start(
+                out=x_first[:, i * piece_rows : (i + 1) * piece_rows, :],
+                in_=x[0, :, i * piece_rows : (i + 1) * piece_rows, :],
+            )
+        for k in range(1, AHEAD):
             load(k)
 
         w_sb = const.tile([P, 4 * C], BF16)
         nc.scalar.dma_start(out=w_sb[:], in_=w_fusion.rearrange("o k a b -> o (k a b)"))
         ident = const.tile([P, P], F32)
         make_identity(nc, ident[:])
-        ident_bf = const.tile([P, P], BF16)
-        make_identity(nc, ident_bf[:])
         w_words = w_sb[:].bitcast(F32).rearrange("o (c u) -> o u c", u=2)
-        a_ps = psa.tile([P, 4 * P], F32)
+        a_ps = psa.tile([P, BANK], F32)
         for u in range(2):
             nc.tensor.transpose(a_ps[:, u * O : (u + 1) * O], w_words[:, u, :], ident[:])
         w_grouped = const.tile([P, 4 * O], BF16, align_bytes=64)
@@ -166,53 +194,61 @@ def tile_haarwaveletlayer_kernel(tc, x, w_fusion, out):
         )
         w_codes = const.tile([P, O], U32, align_bytes=64)
         w_scales = const.tile([P, O], U8, align_bytes=64)
-        flip(2)
-        flip(3)
-        flip_copy(2)
-        flip_copy(3)
+        for half in range(2):
+            flip(("x", 1, half), even_rows(1, half), 4)
+            flip_copy(spool_x, ("x", 1, half), 4)
 
         for k in range(NCH):
             if k + AHEAD < NCH:
                 load(k + AHEAD)
             if k >= 3:
                 emit(k - 3)
-            if k + 1 < NCH:
-                flip_back(2 * k + 2)
-                flip_back(2 * k + 3)
             if k + 2 < NCH:
-                flip(2 * k + 4)
-                flip(2 * k + 5)
-            z_sb = zpool.tile([P, NG, 6, RUN], F32)
-            zt[k] = z_sb
-            if k == 0:
-                vertical_chunk(0, 0, ADD)
-                vertical_chunk(0, 1, SUB)
-                negate(0, 0, NG)
-                nc.vector.quantize_mx(out=w_codes[:].bitcast(FP8X4), scales=w_scales[:], in_=w_grouped[:])
-            else:
                 for half in range(2):
-                    vertical_half(2 * k + half, 0, ADD)
-                    vertical_half(2 * k + half, 1, SUB)
-                    negate(k, HG * half, HG * (half + 1))
-            if k + 2 < NCH:
-                flip_copy(2 * k + 4)
-                flip_copy(2 * k + 5)
-            if k >= 1:
-                horizontal(nc.vector, k - 1, 0, NG - G_GROUPS)
+                    flip(("x", k + 2, half), even_rows(k + 2, half), 4)
+                for half in range(2):
+                    flip_copy(spool_x, ("x", k + 2, half), 4)
+            z_sb = zpool.tile([P, 3, NG, 2, RUN], F32)
+            zt[k] = z_sb
+            for half in range(2):
+                if k == 0:
+                    for i in range(half * HEAD_PIECES // 2, (half + 1) * HEAD_PIECES // 2):
+                        rows = x_first[:, i * piece_rows : (i + 1) * piece_rows, :].rearrange(
+                            "p (i r) w -> p r i w", r=2
+                        )
+                        for v, op in ((0, ADD), (1, SUB)):
+                            vertical(0, rows[:, 0], rows[:, 1], i * NG // HEAD_PIECES, piece_rows // 2, v, op)
+                else:
+                    vertical_half(k, half)
+                if k + 1 < NCH:
+                    flip_back(("x", k + 1, half), 4)
+                negate(k, half * HG, (half + 1) * HG)
+                if half == 0 and k < NCH - 1:
+                    for part in range(2):
+                        flip(("e", k, part), even_columns(k, part), e_blocks(part))
+                    for part in range(2):
+                        flip_copy(spool_e, ("e", k, part), e_blocks(part))
+            if k == 0:
+                nc.vector.quantize_mx(out=w_codes[:].bitcast(FP8X4), scales=w_scales[:], in_=w_grouped[:])
+            for part in range(2):
+                if k >= 1:
+                    horizontal_psum(k - 1, part)
+                if k < NCH - 1:
+                    flip_back(("e", k, part), e_blocks(part))
             if k >= 2:
                 quantise(k - 2, 0, NP)
             g_sb = gpool.tile([P, 4 * NP], BF16, align_bytes=64)
             gt[k] = g_sb
             if k < NCH - 1:
-                horizontal(nc.gpsimd, k, NG - G_GROUPS, NG)
+                horizontal_sbuf(nc.gpsimd, k, V_GROUPS, NG)
 
         last = NCH - 1
         emit(last - 2)
+        horizontal_sbuf(nc.vector, last, 0, HG)
         quantise(last - 1, 0, NP)
         emit(last - 1)
-        horizontal(nc.vector, last, 0, HG)
-        horizontal(nc.vector, last, HG, NG)
-        for h in range(2):
-            quantise(last, h * N_TILE, (h + 1) * N_TILE)
-            multiply(last, h)
-            store(last, h * N_TILE, (h + 1) * N_TILE)
+        horizontal_sbuf(nc.vector, last, HG, NG)
+        for c0, c1 in ((0, 512), (512, 768), (768, 1024)):
+            quantise(last, c0, c1)
+            multiply(last, c0, c1)
+            store(last, c0, c1)

@@ -27,7 +27,7 @@ AHEAD = 3
 HPAIRS = PAIRS // 2
 HG = NG // 2
 BANK_G = BANK // (2 * RUN)
-V_GROUPS = 104
+V_GROUPS = 80
 HEAD_PIECES = 4
 
 FLOPS = 2 * B * (H // 2) * (W // 2) * 4 * C * O

@@ -27,7 +27,7 @@ AHEAD = 3
 HPAIRS = PAIRS // 2
 HG = NG // 2
 BANK_G = BANK // (2 * RUN)
-V_GROUPS = 80
+V_GROUPS = 93
 HEAD_PIECES = 4
 
 FLOPS = 2 * B * (H // 2) * (W // 2) * 4 * C * O

@@ -19,6 +19,7 @@ ROWS = 2 * PAIRS
 NP = PAIRS * (W // 2)
 RUN = 4
 NG = NP // RUN
+PAIR_G = NG // PAIRS
 N_TILE = 512
 BANK = 512
 CHUNKS_PER_IMAGE = H // ROWS
@@ -27,10 +28,33 @@ AHEAD = 3
 HPAIRS = PAIRS // 2
 HG = NG // 2
 BANK_G = BANK // (2 * RUN)
-V_GROUPS = 93
 HEAD_PIECES = 4
+T_PAIRS = 2
+T_FROM = 4
+T_BLOCKS = 2 * T_PAIRS
+HALF_W = W // 2
 
 FLOPS = 2 * B * (H // 2) * (W // 2) * 4 * C * O
+
+
+def t_pairs(k):
+    return T_PAIRS if k >= T_FROM else 0
+
+
+def v_pairs(k):
+    return PAIRS - t_pairs(k)
+
+
+def half_pairs(k, half):
+    return HPAIRS if half == 0 else v_pairs(k) - HPAIRS
+
+
+def n_groups(k):
+    return v_pairs(k) * PAIR_G
+
+
+def v_groups(k):
+    return 81 if t_pairs(k) else 93
 
 
 def tile_haarwaveletlayer_kernel(tc, x, w_fusion, out):
@@ -40,6 +64,7 @@ def tile_haarwaveletlayer_kernel(tc, x, w_fusion, out):
         xin = ctx.enter_context(tc.tile_pool(name="xin", bufs=AHEAD + 1))
         spool_x = ctx.enter_context(tc.tile_pool(name="spool_x", bufs=4))
         spool_e = ctx.enter_context(tc.tile_pool(name="spool_e", bufs=2))
+        tpool = ctx.enter_context(tc.tile_pool(name="tpool", bufs=2))
         zpool = ctx.enter_context(tc.tile_pool(name="zpool", bufs=2))
         gpool = ctx.enter_context(tc.tile_pool(name="gpool", bufs=2))
         qpool = ctx.enter_context(tc.tile_pool(name="qpool", bufs=2))
@@ -51,6 +76,7 @@ def tile_haarwaveletlayer_kernel(tc, x, w_fusion, out):
 
         xe = {}
         xo = {}
+        xb = {}
         at = {}
         st = {}
         bt = {}
@@ -58,16 +84,25 @@ def tile_haarwaveletlayer_kernel(tc, x, w_fusion, out):
         gt = {}
         qt = {}
         ot = {}
+        ht = {}
 
         def load(k):
             n, part = divmod(k, CHUNKS_PER_IMAGE)
-            rows = x[n, :, part * ROWS : (part + 1) * ROWS, :].rearrange("c (i r) w -> c r i w", r=2)
+            r0 = part * ROWS
+            r1 = r0 + 2 * v_pairs(k)
+            rows = x[n, :, r0:r1, :].rearrange("c (i r) w -> c r i w", r=2)
             x_even = xin.tile([P, PAIRS, W], BF16)
-            nc.sync.dma_start(out=x_even[:], in_=rows[:, 0])
+            nc.sync.dma_start(out=x_even[:, 0 : v_pairs(k), :], in_=rows[:, 0])
             xe[k] = x_even
             x_odd = xin.tile([P, PAIRS, W], BF16)
-            nc.sync.dma_start(out=x_odd[:], in_=rows[:, 1])
+            nc.sync.dma_start(out=x_odd[:, 0 : v_pairs(k), :], in_=rows[:, 1])
             xo[k] = x_odd
+            if t_pairs(k):
+                x_blocks = xin.tile([P, 2, 2 * T_PAIRS, HALF_W], BF16)
+                halves = x[n, :, r1 : r0 + ROWS, :].rearrange("c r (h w) -> c h r w", h=2)
+                for h in range(2):
+                    nc.sync.dma_start(out=x_blocks[:, h], in_=halves[:, h])
+                xb[k] = x_blocks
 
         def flip(key, source, blocks):
             a_ps = psa.tile([P, BANK], F32)
@@ -89,15 +124,18 @@ def tile_haarwaveletlayer_kernel(tc, x, w_fusion, out):
         def even_rows(k, half):
             return xe[k][:].rearrange("p i w -> p (i w)").bitcast(F32)[:, half * BANK : (half + 1) * BANK]
 
+        def x_blocks_of(k, half):
+            return half_pairs(k, half) // 2
+
         def even_columns(k, part):
             return zt[k][:, 0].rearrange("p g v e -> p (g v e)")[:, part * BANK : (part + 1) * BANK]
 
-        def e_blocks(part):
-            groups = min(V_GROUPS - part * BANK_G, BANK_G)
+        def e_blocks(k, part):
+            groups = min(v_groups(k) - part * BANK_G, BANK_G)
             return (groups * 2 * RUN + P - 1) // P
 
         def vertical(k, top, bottom, g0, pairs, v, op):
-            zv = zt[k][:, 0:2, g0 : g0 + pairs * (NG // PAIRS)].rearrange("p q (i g) v e -> p v q i g e", i=pairs)
+            zv = zt[k][:, 0:2, g0 : g0 + pairs * PAIR_G].rearrange("p q (i g) v e -> p v q i g e", i=pairs)
             nc.vector.tensor_tensor(
                 out=zv[:, v],
                 in0=top.rearrange("p i (g e q) -> p q i g e", e=RUN, q=2),
@@ -106,10 +144,11 @@ def tile_haarwaveletlayer_kernel(tc, x, w_fusion, out):
             )
 
         def vertical_half(k, half):
-            top = bt["x", k, half][:].bitcast(BF16).rearrange("p (i w) -> p i w", i=HPAIRS)
-            bottom = xo[k][:, half * HPAIRS : (half + 1) * HPAIRS, :]
-            vertical(k, top, bottom, half * HG, HPAIRS, 0, ADD)
-            vertical(k, top, bottom, half * HG, HPAIRS, 1, SUB)
+            pairs = half_pairs(k, half)
+            top = bt["x", k, half][:].bitcast(BF16)[:, 0 : pairs * W].rearrange("p (i w) -> p i w", i=pairs)
+            bottom = xo[k][:, half * HPAIRS : half * HPAIRS + pairs, :]
+            vertical(k, top, bottom, half * HG, pairs, 0, ADD)
+            vertical(k, top, bottom, half * HG, pairs, 1, SUB)
 
         def negate(k, g0, g1):
             nc.scalar.activation(out=zt[k][:, 2, g0:g1], in_=zt[k][:, 1, g0:g1], func=COPY, scale=-1.0)
@@ -127,9 +166,41 @@ def tile_haarwaveletlayer_kernel(tc, x, w_fusion, out):
 
         def horizontal_psum(k, part):
             g0 = part * BANK_G
-            g1 = min(V_GROUPS, g0 + BANK_G)
+            g1 = min(v_groups(k), g0 + BANK_G)
             even = bt["e", k, part][:, 0 : (g1 - g0) * 2 * RUN].rearrange("p (g v e) -> p g v e", v=2, e=RUN)
             horizontal(nc.vector, k, g0, g1, even)
+
+        def haar_flip(k):
+            a_ps = psa.tile([P, 2 * BANK], BF16)
+            for i in range(T_PAIRS):
+                for h in range(2):
+                    b = 2 * i + h
+                    nc.tensor.transpose(
+                        a_ps[:, b * P : (b + 1) * P],
+                        xb[k][:, h, 2 * i : 2 * i + 2, :].rearrange("p r w -> p (r w)"),
+                        ident_bf[:],
+                    )
+            at["t", k] = a_ps
+
+        def haar_copy(k):
+            t_sb = tpool.tile([P, T_BLOCKS * P], BF16)
+            st["t", k] = t_sb
+            nc.scalar.copy(out=t_sb[:], in_=at["t", k][:, 0 : T_BLOCKS * P])
+
+        def haar_multiply(k):
+            acc = psm.tile([P, N_TILE], F32)
+            ht[k] = acc
+            for b in range(T_BLOCKS):
+                nc.tensor.matmul(
+                    out=acc[:, b * P : (b + 1) * P],
+                    lhsT=st["t", k][:, b * P : (b + 1) * P],
+                    rhs=haar[:].rearrange("k j s v -> k (j s v)"),
+                    start=True,
+                    stop=True,
+                )
+
+        def haar_store(k):
+            nc.scalar.copy(out=gt[k][:, 16 * n_groups(k) : 4 * NP], in_=ht[k][:, 0 : T_BLOCKS * P])
 
         def quantise(k, c0, c1):
             if c0 == 0:
@@ -183,6 +254,17 @@ def tile_haarwaveletlayer_kernel(tc, x, w_fusion, out):
         nc.scalar.dma_start(out=w_sb[:], in_=w_fusion.rearrange("o k a b -> o (k a b)"))
         ident = const.tile([P, P], F32)
         make_identity(nc, ident[:])
+        ident_bf = const.tile([P, P], BF16)
+        make_identity(nc, ident_bf[:])
+        cells = ident[:].rearrange("k (r j q) -> k r j q", r=2, q=2)
+        u_sb = const.tile([P, 2, HALF_W // 2, 2], F32)
+        nc.gpsimd.tensor_tensor(out=u_sb[:, 0], in0=cells[:, 0], in1=cells[:, 1], op=ADD)
+        nc.gpsimd.tensor_tensor(out=u_sb[:, 1], in0=cells[:, 0], in1=cells[:, 1], op=SUB)
+        haar = const.tile([P, HALF_W // 2, 2, 2], BF16)
+        columns = u_sb[:].rearrange("k v j q -> k q j v")
+        nc.gpsimd.tensor_tensor(out=haar[:, :, 0, :], in0=columns[:, 0], in1=columns[:, 1], op=ADD)
+        nc.gpsimd.tensor_tensor(out=haar[:, :, 1, :], in0=columns[:, 0], in1=columns[:, 1], op=SUB)
+
         w_words = w_sb[:].bitcast(F32).rearrange("o (c u) -> o u c", u=2)
         a_ps = psa.tile([P, BANK], F32)
         for u in range(2):
@@ -195,19 +277,26 @@ def tile_haarwaveletlayer_kernel(tc, x, w_fusion, out):
         w_codes = const.tile([P, O], U32, align_bytes=64)
         w_scales = const.tile([P, O], U8, align_bytes=64)
         for half in range(2):
-            flip(("x", 1, half), even_rows(1, half), 4)
-            flip_copy(spool_x, ("x", 1, half), 4)
+            flip(("x", 1, half), even_rows(1, half), x_blocks_of(1, half))
+            flip_copy(spool_x, ("x", 1, half), x_blocks_of(1, half))
 
         for k in range(NCH):
             if k + AHEAD < NCH:
                 load(k + AHEAD)
+            if k >= 1 and t_pairs(k - 1):
+                haar_store(k - 1)
             if k >= 3:
                 emit(k - 3)
             if k + 2 < NCH:
                 for half in range(2):
-                    flip(("x", k + 2, half), even_rows(k + 2, half), 4)
+                    flip(("x", k + 2, half), even_rows(k + 2, half), x_blocks_of(k + 2, half))
+            if t_pairs(k):
+                haar_flip(k)
+            if k + 2 < NCH:
                 for half in range(2):
-                    flip_copy(spool_x, ("x", k + 2, half), 4)
+                    flip_copy(spool_x, ("x", k + 2, half), x_blocks_of(k + 2, half))
+            if t_pairs(k):
+                haar_copy(k)
             z_sb = zpool.tile([P, 3, NG, 2, RUN], F32)
             zt[k] = z_sb
             for half in range(2):
@@ -221,33 +310,36 @@ def tile_haarwaveletlayer_kernel(tc, x, w_fusion, out):
                 else:
                     vertical_half(k, half)
                 if k + 1 < NCH:
-                    flip_back(("x", k + 1, half), 4)
-                negate(k, half * HG, (half + 1) * HG)
+                    flip_back(("x", k + 1, half), x_blocks_of(k + 1, half))
+                negate(k, half * HG, half * HG + half_pairs(k, half) * PAIR_G)
                 if half == 0 and k < NCH - 1:
                     for part in range(2):
-                        flip(("e", k, part), even_columns(k, part), e_blocks(part))
+                        flip(("e", k, part), even_columns(k, part), e_blocks(k, part))
                     for part in range(2):
-                        flip_copy(spool_e, ("e", k, part), e_blocks(part))
+                        flip_copy(spool_e, ("e", k, part), e_blocks(k, part))
+            if t_pairs(k):
+                haar_multiply(k)
             if k == 0:
                 nc.vector.quantize_mx(out=w_codes[:].bitcast(FP8X4), scales=w_scales[:], in_=w_grouped[:])
             for part in range(2):
                 if k >= 1:
                     horizontal_psum(k - 1, part)
                 if k < NCH - 1:
-                    flip_back(("e", k, part), e_blocks(part))
+                    flip_back(("e", k, part), e_blocks(k, part))
             if k >= 2:
                 quantise(k - 2, 0, NP)
             g_sb = gpool.tile([P, 4 * NP], BF16, align_bytes=64)
             gt[k] = g_sb
             if k < NCH - 1:
-                horizontal_sbuf(nc.gpsimd, k, V_GROUPS, NG)
+                horizontal_sbuf(nc.gpsimd, k, v_groups(k), n_groups(k))
 
         last = NCH - 1
+        haar_store(last)
         emit(last - 2)
         horizontal_sbuf(nc.vector, last, 0, HG)
         quantise(last - 1, 0, NP)
         emit(last - 1)
-        horizontal_sbuf(nc.vector, last, HG, NG)
+        horizontal_sbuf(nc.vector, last, HG, n_groups(last))
         for c0, c1 in ((0, 512), (512, 768), (768, 1024)):
             quantise(last, c0, c1)
             multiply(last, c0, c1)

@@ -279,6 +279,8 @@ def tile_haarwaveletlayer_kernel(tc, x, w_fusion, out):
         for half in range(2):
             flip(("x", 1, half), even_rows(1, half), x_blocks_of(1, half))
             flip_copy(spool_x, ("x", 1, half), x_blocks_of(1, half))
+        for half in range(2):
+            flip_back(("x", 1, half), x_blocks_of(1, half))
 
         for k in range(NCH):
             if k + AHEAD < NCH:
@@ -309,10 +311,10 @@ def tile_haarwaveletlayer_kernel(tc, x, w_fusion, out):
                             vertical(0, rows[:, 0], rows[:, 1], i * NG // HEAD_PIECES, piece_rows // 2, v, op)
                 else:
                     vertical_half(k, half)
-                if k + 1 < NCH:
+                if 1 <= k < NCH - 1:
                     flip_back(("x", k + 1, half), x_blocks_of(k + 1, half))
                 negate(k, half * HG, half * HG + half_pairs(k, half) * PAIR_G)
-                if half == 0 and k < NCH - 1:
+                if half == 0 and 1 <= k < NCH - 1:
                     for part in range(2):
                         flip(("e", k, part), even_columns(k, part), e_blocks(k, part))
                     for part in range(2):
@@ -322,14 +324,16 @@ def tile_haarwaveletlayer_kernel(tc, x, w_fusion, out):
             if k == 0:
                 nc.vector.quantize_mx(out=w_codes[:].bitcast(FP8X4), scales=w_scales[:], in_=w_grouped[:])
             for part in range(2):
-                if k >= 1:
+                if k >= 2:
                     horizontal_psum(k - 1, part)
-                if k < NCH - 1:
+                if 1 <= k < NCH - 1:
                     flip_back(("e", k, part), e_blocks(k, part))
             if k >= 2:
                 quantise(k - 2, 0, NP)
             g_sb = gpool.tile([P, 4 * NP], BF16, align_bytes=64)
             gt[k] = g_sb
+            if k == 0:
+                horizontal_sbuf(nc.vector, 0, 0, v_groups(0))
             if k < NCH - 1:
                 horizontal_sbuf(nc.gpsimd, k, v_groups(k), n_groups(k))
 

@@ -54,7 +54,7 @@ def n_groups(k):
 
 
 def v_groups(k):
-    return 81 if t_pairs(k) else 93
+    return 80 if t_pairs(k) else 93
 
 
 def tile_haarwaveletlayer_kernel(tc, x, w_fusion, out):

@@ -74,8 +74,7 @@ def tile_haarwaveletlayer_kernel(tc, x, w_fusion, out):
         psm = ctx.enter_context(tc.psum_pool(name="psm", bufs=2))
         ctx.enter_context(tc.manual_schedule())
 
-        xe = {}
-        xo = {}
+        xr = {}
         xb = {}
         at = {}
         st = {}
@@ -90,13 +89,10 @@ def tile_haarwaveletlayer_kernel(tc, x, w_fusion, out):
             n, part = divmod(k, CHUNKS_PER_IMAGE)
             r0 = part * ROWS
             r1 = r0 + 2 * v_pairs(k)
-            rows = x[n, :, r0:r1, :].rearrange("c (i r) w -> c r i w", r=2)
-            x_even = xin.tile([P, PAIRS, W], BF16)
-            nc.sync.dma_start(out=x_even[:, 0 : v_pairs(k), :], in_=rows[:, 0])
-            xe[k] = x_even
-            x_odd = xin.tile([P, PAIRS, W], BF16)
-            nc.sync.dma_start(out=x_odd[:, 0 : v_pairs(k), :], in_=rows[:, 1])
-            xo[k] = x_odd
+            x_rows = xin.tile([P, ROWS, W], BF16)
+            nc.sync.dma_start(out=x_rows[:, 0:PAIRS, :], in_=x[n, :, r0 : r0 + PAIRS, :])
+            nc.sync.dma_start(out=x_rows[:, PAIRS : r1 - r0, :], in_=x[n, :, r0 + PAIRS : r1, :])
+            xr[k] = x_rows
             if t_pairs(k):
                 x_blocks = xin.tile([P, 2, 2 * T_PAIRS, HALF_W], BF16)
                 halves = x[n, :, r1 : r0 + ROWS, :].rearrange("c r (h w) -> c h r w", h=2)
@@ -104,10 +100,10 @@ def tile_haarwaveletlayer_kernel(tc, x, w_fusion, out):
                     nc.sync.dma_start(out=x_blocks[:, h], in_=halves[:, h])
                 xb[k] = x_blocks
 
-        def flip(key, source, blocks):
+        def flip(key, source, blocks, step=P):
             a_ps = psa.tile([P, BANK], F32)
             for b in range(blocks):
-                nc.tensor.transpose(a_ps[:, b * P : (b + 1) * P], source[:, b * P : (b + 1) * P], ident[:])
+                nc.tensor.transpose(a_ps[:, b * P : (b + 1) * P], source[:, b * step : b * step + P], ident[:])
             at[key] = a_ps
 
         def flip_copy(pool, key, blocks):
@@ -121,8 +117,9 @@ def tile_haarwaveletlayer_kernel(tc, x, w_fusion, out):
             for b in range(blocks):
                 nc.tensor.transpose(b_ps[:, b * P : (b + 1) * P], st[key][:, b * P : (b + 1) * P], ident[:])
 
-        def even_rows(k, half):
-            return xe[k][:].rearrange("p i w -> p (i w)").bitcast(F32)[:, half * BANK : (half + 1) * BANK]
+        def middle_rows(k, half):
+            words = xr[k][:].rearrange("p r w -> p (r w)").bitcast(F32)
+            return words[:, 2 * half * BANK + HALF_W : 2 * (half + 1) * BANK]
 
         def x_blocks_of(k, half):
             return half_pairs(k, half) // 2
@@ -145,10 +142,17 @@ def tile_haarwaveletlayer_kernel(tc, x, w_fusion, out):
 
         def vertical_half(k, half):
             pairs = half_pairs(k, half)
-            top = bt["x", k, half][:].bitcast(BF16)[:, 0 : pairs * W].rearrange("p (i w) -> p i w", i=pairs)
-            bottom = xo[k][:, half * HPAIRS : half * HPAIRS + pairs, :]
-            vertical(k, top, bottom, half * HG, pairs, 0, ADD)
-            vertical(k, top, bottom, half * HG, pairs, 1, SUB)
+            split = "p m u (g e q) -> p q m u g e"
+            inner = bt["x", k, half][:].bitcast(BF16)[:, 0 : pairs * W].rearrange("p (m u w) -> p m u w", u=2, w=W)
+            inner = inner.rearrange(split, e=RUN, q=2)
+            fours = xr[k][:, 2 * half * HPAIRS : 2 * (half * HPAIRS + pairs), :].rearrange("p (m f) w -> p m f w", f=4)
+            outer = fours[:, :, 0:4:3, :].rearrange(split, e=RUN, q=2)
+            g0 = half * HG
+            zv = zt[k][:, 0:2, g0 : g0 + pairs * PAIR_G].rearrange("p q (u m g) v e -> p v q m u g e", u=2, g=PAIR_G)
+            for u in range(2):
+                top, bottom = (outer, inner) if u == 0 else (inner, outer)
+                for v, op in ((0, ADD), (1, SUB)):
+                    nc.vector.tensor_tensor(out=zv[:, v, :, :, u], in0=top[:, :, :, u], in1=bottom[:, :, :, u], op=op)
 
         def negate(k, g0, g1):
             nc.scalar.activation(out=zt[k][:, 2, g0:g1], in_=zt[k][:, 1, g0:g1], func=COPY, scale=-1.0)
@@ -227,7 +231,18 @@ def tile_haarwaveletlayer_kernel(tc, x, w_fusion, out):
                 start=True,
                 stop=True,
             )
-            nc.scalar.activation(out=ot[k][:, c0:c1], in_=acc[:, 0 : c1 - c0], func=COPY, scale=0.5)
+            if k == 0:
+                nc.scalar.activation(out=ot[k][:, c0:c1], in_=acc[:, 0 : c1 - c0], func=COPY, scale=0.5)
+            else:
+                n = half_pairs(k, c0 // N_TILE) * HALF_W
+                nc.scalar.activation(
+                    out=ot[k][:, c0 : c0 + n].rearrange("p (m u j) -> p u m j", u=2, j=HALF_W),
+                    in_=acc[:, 0:n].rearrange("p (u m j) -> p u m j", u=2, j=HALF_W),
+                    func=COPY,
+                    scale=0.5,
+                )
+                if n < N_TILE:
+                    nc.scalar.activation(out=ot[k][:, c0 + n : c1], in_=acc[:, n:N_TILE], func=COPY, scale=0.5)
 
         def store(k, c0, c1):
             n, part = divmod(k, CHUNKS_PER_IMAGE)
@@ -277,7 +292,7 @@ def tile_haarwaveletlayer_kernel(tc, x, w_fusion, out):
         w_codes = const.tile([P, O], U32, align_bytes=64)
         w_scales = const.tile([P, O], U8, align_bytes=64)
         for half in range(2):
-            flip(("x", 1, half), even_rows(1, half), x_blocks_of(1, half))
+            flip(("x", 1, half), middle_rows(1, half), x_blocks_of(1, half), 2 * P)
             flip_copy(spool_x, ("x", 1, half), x_blocks_of(1, half))
         for half in range(2):
             flip_back(("x", 1, half), x_blocks_of(1, half))
@@ -291,7 +306,7 @@ def tile_haarwaveletlayer_kernel(tc, x, w_fusion, out):
                 emit(k - 3)
             if k + 2 < NCH:
                 for half in range(2):
-                    flip(("x", k + 2, half), even_rows(k + 2, half), x_blocks_of(k + 2, half))
+                    flip(("x", k + 2, half), middle_rows(k + 2, half), x_blocks_of(k + 2, half), 2 * P)
             if t_pairs(k):
                 haar_flip(k)
             if k + 2 < NCH:
@@ -344,7 +359,7 @@ def tile_haarwaveletlayer_kernel(tc, x, w_fusion, out):
         quantise(last - 1, 0, NP)
         emit(last - 1)
         horizontal_sbuf(nc.vector, last, HG, n_groups(last))
-        for c0, c1 in ((0, 512), (512, 768), (768, 1024)):
+        for c0, c1 in ((0, 512), (512, 1024)):
             quantise(last, c0, c1)
             multiply(last, c0, c1)
             store(last, c0, c1)

@@ -65,7 +65,7 @@ def tile_haarwaveletlayer_kernel(tc, x, w_fusion, out):
         spool_x = ctx.enter_context(tc.tile_pool(name="spool_x", bufs=4))
         spool_e = ctx.enter_context(tc.tile_pool(name="spool_e", bufs=2))
         tpool = ctx.enter_context(tc.tile_pool(name="tpool", bufs=2))
-        zpool = ctx.enter_context(tc.tile_pool(name="zpool", bufs=2))
+        zpool = ctx.enter_context(tc.tile_pool(name="zpool", bufs=3))
         gpool = ctx.enter_context(tc.tile_pool(name="gpool", bufs=2))
         qpool = ctx.enter_context(tc.tile_pool(name="qpool", bufs=2))
         opool = ctx.enter_context(tc.tile_pool(name="opool", bufs=3))
@@ -291,11 +291,12 @@ def tile_haarwaveletlayer_kernel(tc, x, w_fusion, out):
         )
         w_codes = const.tile([P, O], U32, align_bytes=64)
         w_scales = const.tile([P, O], U8, align_bytes=64)
-        for half in range(2):
-            flip(("x", 1, half), middle_rows(1, half), x_blocks_of(1, half), 2 * P)
-            flip_copy(spool_x, ("x", 1, half), x_blocks_of(1, half))
-        for half in range(2):
-            flip_back(("x", 1, half), x_blocks_of(1, half))
+
+        def turn(k):
+            for half in range(2):
+                flip(("x", k, half), middle_rows(k, half), x_blocks_of(k, half), 2 * P)
+            for half in range(2):
+                flip_copy(spool_x, ("x", k, half), x_blocks_of(k, half))
 
         for k in range(NCH):
             if k + AHEAD < NCH:
@@ -304,12 +305,12 @@ def tile_haarwaveletlayer_kernel(tc, x, w_fusion, out):
                 haar_store(k - 1)
             if k >= 3:
                 emit(k - 3)
-            if k + 2 < NCH:
+            if 1 <= k < NCH - 2:
                 for half in range(2):
                     flip(("x", k + 2, half), middle_rows(k + 2, half), x_blocks_of(k + 2, half), 2 * P)
             if t_pairs(k):
                 haar_flip(k)
-            if k + 2 < NCH:
+            if 1 <= k < NCH - 2:
                 for half in range(2):
                     flip_copy(spool_x, ("x", k + 2, half), x_blocks_of(k + 2, half))
             if t_pairs(k):
@@ -329,6 +330,10 @@ def tile_haarwaveletlayer_kernel(tc, x, w_fusion, out):
                 if 1 <= k < NCH - 1:
                     flip_back(("x", k + 1, half), x_blocks_of(k + 1, half))
                 negate(k, half * HG, half * HG + half_pairs(k, half) * PAIR_G)
+                if k == 0 and half == 0:
+                    turn(1)
+                    for h in range(2):
+                        flip_back(("x", 1, h), x_blocks_of(1, h))
                 if half == 0 and 1 <= k < NCH - 1:
                     for part in range(2):
                         flip(("e", k, part), even_columns(k, part), e_blocks(k, part))
@@ -351,6 +356,8 @@ def tile_haarwaveletlayer_kernel(tc, x, w_fusion, out):
                 horizontal_sbuf(nc.vector, 0, 0, v_groups(0))
             if k < NCH - 1:
                 horizontal_sbuf(nc.gpsimd, k, v_groups(k), n_groups(k))
+            if k == 0:
+                turn(2)
 
         last = NCH - 1
         haar_store(last)

@@ -54,7 +54,13 @@ def n_groups(k):
 
 
 def v_groups(k):
+    if k == NCH - 1:
+        return 160
     return 80 if t_pairs(k) else 93
+
+
+def parts(k):
+    return (v_groups(k) + BANK_G - 1) // BANK_G
 
 
 def tile_haarwaveletlayer_kernel(tc, x, w_fusion, out):
@@ -63,7 +69,7 @@ def tile_haarwaveletlayer_kernel(tc, x, w_fusion, out):
         const = ctx.enter_context(tc.tile_pool(name="const", bufs=1))
         xin = ctx.enter_context(tc.tile_pool(name="xin", bufs=AHEAD + 1))
         spool_x = ctx.enter_context(tc.tile_pool(name="spool_x", bufs=4))
-        spool_e = ctx.enter_context(tc.tile_pool(name="spool_e", bufs=2))
+        spool_e = ctx.enter_context(tc.tile_pool(name="spool_e", bufs=3))
         tpool = ctx.enter_context(tc.tile_pool(name="tpool", bufs=2))
         zpool = ctx.enter_context(tc.tile_pool(name="zpool", bufs=3))
         gpool = ctx.enter_context(tc.tile_pool(name="gpool", bufs=2))
@@ -334,11 +340,15 @@ def tile_haarwaveletlayer_kernel(tc, x, w_fusion, out):
                     turn(1)
                     for h in range(2):
                         flip_back(("x", 1, h), x_blocks_of(1, h))
-                if half == 0 and 1 <= k < NCH - 1:
-                    for part in range(2):
+                if k >= 1:
+                    ready = range(2 * half, min(2 * half + 2, parts(k)))
+                    for part in ready:
                         flip(("e", k, part), even_columns(k, part), e_blocks(k, part))
-                    for part in range(2):
+                    for part in ready:
                         flip_copy(spool_e, ("e", k, part), e_blocks(k, part))
+                    if k == NCH - 1:
+                        for part in ready:
+                            flip_back(("e", k, part), e_blocks(k, part))
             if t_pairs(k):
                 haar_multiply(k)
             if k == 0:
@@ -350,22 +360,22 @@ def tile_haarwaveletlayer_kernel(tc, x, w_fusion, out):
                     flip_back(("e", k, part), e_blocks(k, part))
             if k >= 2:
                 quantise(k - 2, 0, NP)
+            if k == NCH - 1:
+                quantise(k - 1, 0, NP)
             g_sb = gpool.tile([P, 4 * NP], BF16, align_bytes=64)
             gt[k] = g_sb
             if k == 0:
                 horizontal_sbuf(nc.vector, 0, 0, v_groups(0))
-            if k < NCH - 1:
-                horizontal_sbuf(nc.gpsimd, k, v_groups(k), n_groups(k))
+            horizontal_sbuf(nc.gpsimd, k, v_groups(k), n_groups(k))
             if k == 0:
                 turn(2)
 
         last = NCH - 1
         haar_store(last)
         emit(last - 2)
-        horizontal_sbuf(nc.vector, last, 0, HG)
-        quantise(last - 1, 0, NP)
         emit(last - 1)
-        horizontal_sbuf(nc.vector, last, HG, n_groups(last))
+        for part in range(parts(last)):
+            horizontal_psum(last, part)
         for c0, c1 in ((0, 512), (512, 1024)):
             quantise(last, c0, c1)
             multiply(last, c0, c1)

@@ -174,6 +174,11 @@ def tile_haarwaveletlayer_kernel(tc, x, w_fusion, out):
         def horizontal_sbuf(engine, k, g0, g1):
             horizontal(engine, k, g0, g1, zt[k][:, 0, g0:g1])
 
+        def horizontal_gpsimd(k, g0, g1):
+            bands = gt[k][:, 16 * g0 : 16 * g1].rearrange("p (g e s v) -> p s g v e", e=RUN, s=2, v=2)
+            for s, op in ((0, ADD), (1, SUB)):
+                nc.gpsimd.tensor_tensor(out=bands[:, s], in0=zt[k][:, 0, g0:g1], in1=zt[k][:, 1, g0:g1], op=op)
+
         def horizontal_psum(k, part):
             g0 = part * BANK_G
             g1 = min(v_groups(k), g0 + BANK_G)
@@ -335,7 +340,8 @@ def tile_haarwaveletlayer_kernel(tc, x, w_fusion, out):
                     vertical_half(k, half)
                 if 1 <= k < NCH - 1:
                     flip_back(("x", k + 1, half), x_blocks_of(k + 1, half))
-                negate(k, half * HG, half * HG + half_pairs(k, half) * PAIR_G)
+                if v_groups(k) > half * HG:
+                    negate(k, half * HG, min(v_groups(k), half * HG + HG))
                 if k == 0 and half == 0:
                     turn(1)
                     for h in range(2):
@@ -366,7 +372,7 @@ def tile_haarwaveletlayer_kernel(tc, x, w_fusion, out):
             gt[k] = g_sb
             if k == 0:
                 horizontal_sbuf(nc.vector, 0, 0, v_groups(0))
-            horizontal_sbuf(nc.gpsimd, k, v_groups(k), n_groups(k))
+            horizontal_gpsimd(k, v_groups(k), n_groups(k))
             if k == 0:
                 turn(2)
 

@@ -56,7 +56,7 @@ def n_groups(k):
 def v_groups(k):
     if k == NCH - 1:
         return 160
-    return 80 if t_pairs(k) else 93
+    return 88 if t_pairs(k) else 93
 
 
 def parts(k):

@@ -28,7 +28,7 @@ AHEAD = 3
 HPAIRS = PAIRS // 2
 HG = NG // 2
 BANK_G = BANK // (2 * RUN)
-HEAD_PIECES = 4
+HEAD_ROWS = ((0, 4), (4, 8), (8, 16), (16, 32))
 T_PAIRS = 2
 T_FROM = 4
 T_BLOCKS = 2 * T_PAIRS
@@ -137,6 +137,16 @@ def tile_haarwaveletlayer_kernel(tc, x, w_fusion, out):
             groups = min(v_groups(k) - part * BANK_G, BANK_G)
             return (groups * 2 * RUN + P - 1) // P
 
+        def even_flips(k, ready):
+            for part in ready:
+                flip(("e", k, part), even_columns(k, part), e_blocks(k, part))
+            for part in ready:
+                flip_copy(spool_e, ("e", k, part), e_blocks(k, part))
+
+        def even_backs(k, ready):
+            for part in ready:
+                flip_back(("e", k, part), e_blocks(k, part))
+
         def vertical(k, top, bottom, g0, pairs, v, op):
             zv = zt[k][:, 0:2, g0 : g0 + pairs * PAIR_G].rearrange("p q (i g) v e -> p v q i g e", i=pairs)
             nc.vector.tensor_tensor(
@@ -227,14 +237,25 @@ def tile_haarwaveletlayer_kernel(tc, x, w_fusion, out):
                 out=codes[:, c0:c1].bitcast(FP8X4), scales=scales[:, c0:c1], in_=gt[k][:, 4 * c0 : 4 * c1]
             )
 
-        def multiply(k, c0, c1):
+        def take_out(by_vector, out, in_):
+            if by_vector:
+                nc.vector.tensor_scalar_mul(out, in_, 0.5)
+            else:
+                nc.scalar.activation(out=out, in_=in_, func=COPY, scale=0.5)
+
+        def multiply(k, c0, c1, spare=False, by_vector=False):
             codes, scales = qt[k]
             if c0 == 0:
                 o_sb = opool.tile([P, NP], F32)
                 ot[k] = o_sb
-            acc = psm.tile([P, N_TILE], F32)
+            if spare:
+                a_ps = psa.tile([P, BANK], F32)
+                bank = a_ps
+            else:
+                acc = psm.tile([P, N_TILE], F32)
+                bank = acc
             nc.tensor.matmul_mx(
-                out=acc[:, 0 : c1 - c0],
+                out=bank[:, 0 : c1 - c0],
                 lhsT=w_codes[:].bitcast(FP8X4),
                 lhsT_scale=w_scales[:],
                 rhs=codes[:, c0:c1].bitcast(FP8X4),
@@ -243,36 +264,31 @@ def tile_haarwaveletlayer_kernel(tc, x, w_fusion, out):
                 stop=True,
             )
             if k == 0:
-                nc.scalar.activation(out=ot[k][:, c0:c1], in_=acc[:, 0 : c1 - c0], func=COPY, scale=0.5)
+                take_out(by_vector, ot[k][:, c0:c1], bank[:, 0 : c1 - c0])
             else:
                 n = half_pairs(k, c0 // N_TILE) * HALF_W
-                nc.scalar.activation(
-                    out=ot[k][:, c0 : c0 + n].rearrange("p (m u j) -> p u m j", u=2, j=HALF_W),
-                    in_=acc[:, 0:n].rearrange("p (u m j) -> p u m j", u=2, j=HALF_W),
-                    func=COPY,
-                    scale=0.5,
+                take_out(
+                    by_vector,
+                    ot[k][:, c0 : c0 + n].rearrange("p (m u j) -> p u m j", u=2, j=HALF_W),
+                    bank[:, 0:n].rearrange("p (u m j) -> p u m j", u=2, j=HALF_W),
                 )
                 if n < N_TILE:
-                    nc.scalar.activation(out=ot[k][:, c0 + n : c1], in_=acc[:, n:N_TILE], func=COPY, scale=0.5)
+                    take_out(by_vector, ot[k][:, c0 + n : c1], bank[:, n:N_TILE])
 
-        def store(k, c0, c1):
+        def store(k, c0, c1, queue=nc.scalar):
             n, part = divmod(k, CHUNKS_PER_IMAGE)
             i0 = part * PAIRS + c0 // (W // 2)
             i1 = part * PAIRS + c1 // (W // 2)
-            nc.scalar.dma_start(out=out[n, :, i0:i1, :].rearrange("o i j -> o (i j)"), in_=ot[k][:, c0:c1])
+            queue.dma_start(out=out[n, :, i0:i1, :].rearrange("o i j -> o (i j)"), in_=ot[k][:, c0:c1])
 
-        def emit(k):
-            multiply(k, 0, N_TILE)
-            multiply(k, N_TILE, NP)
-            store(k, 0, NP)
+        def emit(k, spare=False, queue=nc.scalar):
+            multiply(k, 0, N_TILE, spare)
+            multiply(k, N_TILE, NP, spare)
+            store(k, 0, NP, queue)
 
         x_first = const.tile([P, ROWS, W], BF16)
-        piece_rows = ROWS // HEAD_PIECES
-        for i in range(HEAD_PIECES):
-            nc.sync.dma_start(
-                out=x_first[:, i * piece_rows : (i + 1) * piece_rows, :],
-                in_=x[0, :, i * piece_rows : (i + 1) * piece_rows, :],
-            )
+        for r0, r1 in HEAD_ROWS:
+            nc.sync.dma_start(out=x_first[:, r0:r1, :], in_=x[0, :, r0:r1, :])
         for k in range(1, AHEAD):
             load(k)
 
@@ -330,12 +346,11 @@ def tile_haarwaveletlayer_kernel(tc, x, w_fusion, out):
             zt[k] = z_sb
             for half in range(2):
                 if k == 0:
-                    for i in range(half * HEAD_PIECES // 2, (half + 1) * HEAD_PIECES // 2):
-                        rows = x_first[:, i * piece_rows : (i + 1) * piece_rows, :].rearrange(
-                            "p (i r) w -> p r i w", r=2
-                        )
-                        for v, op in ((0, ADD), (1, SUB)):
-                            vertical(0, rows[:, 0], rows[:, 1], i * NG // HEAD_PIECES, piece_rows // 2, v, op)
+                    for r0, r1 in HEAD_ROWS:
+                        if r0 // PAIRS == half:
+                            rows = x_first[:, r0:r1, :].rearrange("p (i r) w -> p r i w", r=2)
+                            for v, op in ((0, ADD), (1, SUB)):
+                                vertical(0, rows[:, 0], rows[:, 1], r0 // 2 * PAIR_G, (r1 - r0) // 2, v, op)
                 else:
                     vertical_half(k, half)
                 if 1 <= k < NCH - 1:
@@ -348,28 +363,28 @@ def tile_haarwaveletlayer_kernel(tc, x, w_fusion, out):
                         flip_back(("x", 1, h), x_blocks_of(1, h))
                 if k >= 1:
                     ready = range(2 * half, min(2 * half + 2, parts(k)))
-                    for part in ready:
-                        flip(("e", k, part), even_columns(k, part), e_blocks(k, part))
-                    for part in ready:
-                        flip_copy(spool_e, ("e", k, part), e_blocks(k, part))
-                    if k == NCH - 1:
-                        for part in ready:
-                            flip_back(("e", k, part), e_blocks(k, part))
+                    even_flips(k, ready)
+                    if k == NCH - 1 and half == 0:
+                        even_backs(k, ready)
             if t_pairs(k):
                 haar_multiply(k)
             if k == 0:
                 nc.vector.quantize_mx(out=w_codes[:].bitcast(FP8X4), scales=w_scales[:], in_=w_grouped[:])
-            for part in range(2):
-                if k >= 2:
+            if k >= 2:
+                for part in range(parts(k - 1)):
                     horizontal_psum(k - 1, part)
-                if 1 <= k < NCH - 1:
-                    flip_back(("e", k, part), e_blocks(k, part))
+            if 1 <= k < NCH - 1:
+                even_backs(k, range(parts(k)))
             if k >= 2:
                 quantise(k - 2, 0, NP)
             if k == NCH - 1:
                 quantise(k - 1, 0, NP)
             g_sb = gpool.tile([P, 4 * NP], BF16, align_bytes=64)
             gt[k] = g_sb
+            if k == NCH - 1:
+                haar_store(k)
+                emit(k - 2, queue=nc.sync)
+                even_backs(k, ready)
             if k == 0:
                 horizontal_sbuf(nc.vector, 0, 0, v_groups(0))
             horizontal_gpsimd(k, v_groups(k), n_groups(k))
@@ -377,12 +392,10 @@ def tile_haarwaveletlayer_kernel(tc, x, w_fusion, out):
                 turn(2)
 
         last = NCH - 1
-        haar_store(last)
-        emit(last - 2)
-        emit(last - 1)
+        emit(last - 1, spare=True, queue=nc.sync)
         for part in range(parts(last)):
             horizontal_psum(last, part)
-        for c0, c1 in ((0, 512), (512, 1024)):
-            quantise(last, c0, c1)
-            multiply(last, c0, c1)
-            store(last, c0, c1)
+        for c0, by_vector in ((0, False), (N_TILE, True)):
+            quantise(last, c0, c0 + N_TILE)
+            multiply(last, c0, c0 + N_TILE, by_vector=by_vector)
+            store(last, c0, c0 + N_TILE, nc.sync)

@@ -56,7 +56,7 @@ def n_groups(k):
 def v_groups(k):
     if k == NCH - 1:
         return 160
-    return 88 if t_pairs(k) else 93
+    return 88 if t_pairs(k) else 112
 
 
 def parts(k):
@@ -213,7 +213,7 @@ def tile_haarwaveletlayer_kernel(tc, x, w_fusion, out):
             nc.scalar.copy(out=t_sb[:], in_=at["t", k][:, 0 : T_BLOCKS * P])
 
         def haar_multiply(k):
-            acc = psm.tile([P, N_TILE], F32)
+            acc = psm.tile([P, 2 * N_TILE], BF16)
             ht[k] = acc
             for b in range(T_BLOCKS):
                 nc.tensor.matmul(

from contextlib import ExitStack

import concourse.mybir as mybir
from concourse.masks import make_identity

FP8X4 = mybir.dt.float8_e4m3fn_x4
BF16 = mybir.dt.bfloat16
F32 = mybir.dt.float32
U32 = mybir.dt.uint32
U8 = mybir.dt.uint8
ADD = mybir.AluOpType.add
SUB = mybir.AluOpType.subtract
COPY = mybir.ActivationFunctionType.Copy

P = 128
B, C, H, W, O = 4, 128, 128, 128, 128
PAIRS = 16
ROWS = 2 * PAIRS
NP = PAIRS * (W // 2)
RUN = 4
NG = NP // RUN
PAIR_G = NG // PAIRS
N_TILE = 512
BANK = 512
CHUNKS_PER_IMAGE = H // ROWS
NCH = B * CHUNKS_PER_IMAGE
AHEAD = 3
HPAIRS = PAIRS // 2
HG = NG // 2
BANK_G = BANK // (2 * RUN)
HEAD_ROWS = ((0, 4), (4, 8), (8, 16), (16, 32))
T_PAIRS = 2
T_FROM = 4
T_BLOCKS = 2 * T_PAIRS
HALF_W = W // 2

FLOPS = 2 * B * (H // 2) * (W // 2) * 4 * C * O


def t_pairs(k):
    return T_PAIRS if k >= T_FROM else 0


def v_pairs(k):
    return PAIRS - t_pairs(k)


def half_pairs(k, half):
    return HPAIRS if half == 0 else v_pairs(k) - HPAIRS


def n_groups(k):
    return v_pairs(k) * PAIR_G


def v_groups(k):
    if k == NCH - 1:
        return 160
    return 88 if t_pairs(k) else 112


def parts(k):
    return (v_groups(k) + BANK_G - 1) // BANK_G


def tile_haarwaveletlayer_kernel(tc, x, w_fusion, out):
    nc = tc.nc
    with ExitStack() as ctx:
        const = ctx.enter_context(tc.tile_pool(name="const", bufs=1))
        xin = ctx.enter_context(tc.tile_pool(name="xin", bufs=AHEAD + 1))
        spool_x = ctx.enter_context(tc.tile_pool(name="spool_x", bufs=4))
        spool_e = ctx.enter_context(tc.tile_pool(name="spool_e", bufs=3))
        tpool = ctx.enter_context(tc.tile_pool(name="tpool", bufs=2))
        zpool = ctx.enter_context(tc.tile_pool(name="zpool", bufs=3))
        gpool = ctx.enter_context(tc.tile_pool(name="gpool", bufs=2))
        qpool = ctx.enter_context(tc.tile_pool(name="qpool", bufs=2))
        opool = ctx.enter_context(tc.tile_pool(name="opool", bufs=3))
        psa = ctx.enter_context(tc.psum_pool(name="psa", bufs=2))
        psb = ctx.enter_context(tc.psum_pool(name="psb", bufs=4))
        psm = ctx.enter_context(tc.psum_pool(name="psm", bufs=2))
        ctx.enter_context(tc.manual_schedule())

        xr = {}
        xb = {}
        at = {}
        st = {}
        bt = {}
        zt = {}
        gt = {}
        qt = {}
        ot = {}
        ht = {}

        def load(k):
            n, part = divmod(k, CHUNKS_PER_IMAGE)
            r0 = part * ROWS
            r1 = r0 + 2 * v_pairs(k)
            x_rows = xin.tile([P, ROWS, W], BF16)
            nc.sync.dma_start(out=x_rows[:, 0:PAIRS, :], in_=x[n, :, r0 : r0 + PAIRS, :])
            nc.sync.dma_start(out=x_rows[:, PAIRS : r1 - r0, :], in_=x[n, :, r0 + PAIRS : r1, :])
            xr[k] = x_rows
            if t_pairs(k):
                x_blocks = xin.tile([P, 2, 2 * T_PAIRS, HALF_W], BF16)
                halves = x[n, :, r1 : r0 + ROWS, :].rearrange("c r (h w) -> c h r w", h=2)
                for h in range(2):
                    nc.sync.dma_start(out=x_blocks[:, h], in_=halves[:, h])
                xb[k] = x_blocks

        def flip(key, source, blocks, step=P):
            a_ps = psa.tile([P, BANK], F32)
            for b in range(blocks):
                nc.tensor.transpose(a_ps[:, b * P : (b + 1) * P], source[:, b * step : b * step + P], ident[:])
            at[key] = a_ps

        def flip_copy(pool, key, blocks):
            s_sb = pool.tile([P, BANK], F32)
            st[key] = s_sb
            nc.scalar.copy(out=s_sb[:, 0 : blocks * P], in_=at[key][:, 0 : blocks * P])

        def flip_back(key, blocks):
            b_ps = psb.tile([P, BANK], F32)
            bt[key] = b_ps
            for b in range(blocks):
                nc.tensor.transpose(b_ps[:, b * P : (b + 1) * P], st[key][:, b * P : (b + 1) * P], ident[:])

        def middle_rows(k, half):
            words = xr[k][:].rearrange("p r w -> p (r w)").bitcast(F32)
            return words[:, 2 * half * BANK + HALF_W : 2 * (half + 1) * BANK]

        def x_blocks_of(k, half):
            return half_pairs(k, half) // 2

        def even_columns(k, part):
            return zt[k][:, 0].rearrange("p g v e -> p (g v e)")[:, part * BANK : (part + 1) * BANK]

        def e_blocks(k, part):
            groups = min(v_groups(k) - part * BANK_G, BANK_G)
            return (groups * 2 * RUN + P - 1) // P

        def even_flips(k, ready):
            for part in ready:
                flip(("e", k, part), even_columns(k, part), e_blocks(k, part))
            for part in ready:
                flip_copy(spool_e, ("e", k, part), e_blocks(k, part))

        def even_backs(k, ready):
            for part in ready:
                flip_back(("e", k, part), e_blocks(k, part))

        def vertical(k, top, bottom, g0, pairs, v, op):
            zv = zt[k][:, 0:2, g0 : g0 + pairs * PAIR_G].rearrange("p q (i g) v e -> p v q i g e", i=pairs)
            nc.vector.tensor_tensor(
                out=zv[:, v],
                in0=top.rearrange("p i (g e q) -> p q i g e", e=RUN, q=2),
                in1=bottom.rearrange("p i (g e q) -> p q i g e", e=RUN, q=2),
                op=op,
            )

        def vertical_half(k, half):
            pairs = half_pairs(k, half)
            split = "p m u (g e q) -> p q m u g e"
            inner = bt["x", k, half][:].bitcast(BF16)[:, 0 : pairs * W].rearrange("p (m u w) -> p m u w", u=2, w=W)
            inner = inner.rearrange(split, e=RUN, q=2)
            fours = xr[k][:, 2 * half * HPAIRS : 2 * (half * HPAIRS + pairs), :].rearrange("p (m f) w -> p m f w", f=4)
            outer = fours[:, :, 0:4:3, :].rearrange(split, e=RUN, q=2)
            g0 = half * HG
            zv = zt[k][:, 0:2, g0 : g0 + pairs * PAIR_G].rearrange("p q (u m g) v e -> p v q m u g e", u=2, g=PAIR_G)
            for u in range(2):
                top, bottom = (outer, inner) if u == 0 else (inner, outer)
                for v, op in ((0, ADD), (1, SUB)):
                    nc.vector.tensor_tensor(out=zv[:, v, :, :, u], in0=top[:, :, :, u], in1=bottom[:, :, :, u], op=op)

        def negate(k, g0, g1):
            nc.scalar.activation(out=zt[k][:, 2, g0:g1], in_=zt[k][:, 1, g0:g1], func=COPY, scale=-1.0)

        def horizontal(engine, k, g0, g1, even):
            engine.tensor_tensor(
                out=gt[k][:, 16 * g0 : 16 * g1].rearrange("p (g e s v) -> p g s v e", e=RUN, s=2, v=2),
                in0=even.unsqueeze(2).to_broadcast([P, g1 - g0, 2, 2, RUN]),
                in1=zt[k][:, 1:3, g0:g1].rearrange("p s g v e -> p g s v e"),
                op=ADD,
            )

        def horizontal_sbuf(engine, k, g0, g1):
            horizontal(engine, k, g0, g1, zt[k][:, 0, g0:g1])

        def horizontal_gpsimd(k, g0, g1):
            bands = gt[k][:, 16 * g0 : 16 * g1].rearrange("p (g e s v) -> p s g v e", e=RUN, s=2, v=2)
            for s, op in ((0, ADD), (1, SUB)):
                nc.gpsimd.tensor_tensor(out=bands[:, s], in0=zt[k][:, 0, g0:g1], in1=zt[k][:, 1, g0:g1], op=op)

        def horizontal_psum(k, part):
            g0 = part * BANK_G
            g1 = min(v_groups(k), g0 + BANK_G)
            even = bt["e", k, part][:, 0 : (g1 - g0) * 2 * RUN].rearrange("p (g v e) -> p g v e", v=2, e=RUN)
            horizontal(nc.vector, k, g0, g1, even)

        def haar_flip(k):
            a_ps = psa.tile([P, 2 * BANK], BF16)
            for i in range(T_PAIRS):
                for h in range(2):
                    b = 2 * i + h
                    nc.tensor.transpose(
                        a_ps[:, b * P : (b + 1) * P],
                        xb[k][:, h, 2 * i : 2 * i + 2, :].rearrange("p r w -> p (r w)"),
                        ident_bf[:],
                    )
            at["t", k] = a_ps

        def haar_copy(k):
            t_sb = tpool.tile([P, T_BLOCKS * P], BF16)
            st["t", k] = t_sb
            nc.scalar.copy(out=t_sb[:], in_=at["t", k][:, 0 : T_BLOCKS * P])

        def haar_multiply(k):
            acc = psm.tile([P, 2 * N_TILE], BF16)
            ht[k] = acc
            for b in range(T_BLOCKS):
                nc.tensor.matmul(
                    out=acc[:, b * P : (b + 1) * P],
                    lhsT=st["t", k][:, b * P : (b + 1) * P],
                    rhs=haar[:].rearrange("k j s v -> k (j s v)"),
                    start=True,
                    stop=True,
                )

        def haar_store(k):
            nc.scalar.copy(out=gt[k][:, 16 * n_groups(k) : 4 * NP], in_=ht[k][:, 0 : T_BLOCKS * P])

        def quantise(k, c0, c1):
            if c0 == 0:
                codes = qpool.tile([P, NP], U32, align_bytes=64)
                scales = qpool.tile([P, NP], U8, align_bytes=64)
                qt[k] = (codes, scales)
            codes, scales = qt[k]
            nc.vector.quantize_mx(
                out=codes[:, c0:c1].bitcast(FP8X4), scales=scales[:, c0:c1], in_=gt[k][:, 4 * c0 : 4 * c1]
            )

        def take_out(by_vector, out, in_):
            if by_vector:
                nc.vector.tensor_scalar_mul(out, in_, 0.5)
            else:
                nc.scalar.activation(out=out, in_=in_, func=COPY, scale=0.5)

        def multiply(k, c0, c1, spare=False, by_vector=False):
            codes, scales = qt[k]
            if c0 == 0:
                o_sb = opool.tile([P, NP], F32)
                ot[k] = o_sb
            if spare:
                a_ps = psa.tile([P, BANK], F32)
                bank = a_ps
            else:
                acc = psm.tile([P, N_TILE], F32)
                bank = acc
            nc.tensor.matmul_mx(
                out=bank[:, 0 : c1 - c0],
                lhsT=w_codes[:].bitcast(FP8X4),
                lhsT_scale=w_scales[:],
                rhs=codes[:, c0:c1].bitcast(FP8X4),
                rhs_scale=scales[:, c0:c1],
                start=True,
                stop=True,
            )
            if k == 0:
                take_out(by_vector, ot[k][:, c0:c1], bank[:, 0 : c1 - c0])
            else:
                n = half_pairs(k, c0 // N_TILE) * HALF_W
                take_out(
                    by_vector,
                    ot[k][:, c0 : c0 + n].rearrange("p (m u j) -> p u m j", u=2, j=HALF_W),
                    bank[:, 0:n].rearrange("p (u m j) -> p u m j", u=2, j=HALF_W),
                )
                if n < N_TILE:
                    take_out(by_vector, ot[k][:, c0 + n : c1], bank[:, n:N_TILE])

        def store(k, c0, c1, queue=nc.scalar):
            n, part = divmod(k, CHUNKS_PER_IMAGE)
            i0 = part * PAIRS + c0 // (W // 2)
            i1 = part * PAIRS + c1 // (W // 2)
            queue.dma_start(out=out[n, :, i0:i1, :].rearrange("o i j -> o (i j)"), in_=ot[k][:, c0:c1])

        def emit(k, spare=False, queue=nc.scalar):
            multiply(k, 0, N_TILE, spare)
            multiply(k, N_TILE, NP, spare)
            store(k, 0, NP, queue)

        x_first = const.tile([P, ROWS, W], BF16)
        for r0, r1 in HEAD_ROWS:
            nc.sync.dma_start(out=x_first[:, r0:r1, :], in_=x[0, :, r0:r1, :])
        for k in range(1, AHEAD):
            load(k)

        w_sb = const.tile([P, 4 * C], BF16)
        nc.scalar.dma_start(out=w_sb[:], in_=w_fusion.rearrange("o k a b -> o (k a b)"))
        ident = const.tile([P, P], F32)
        make_identity(nc, ident[:])
        ident_bf = const.tile([P, P], BF16)
        make_identity(nc, ident_bf[:])
        cells = ident[:].rearrange("k (r j q) -> k r j q", r=2, q=2)
        u_sb = const.tile([P, 2, HALF_W // 2, 2], F32)
        nc.gpsimd.tensor_tensor(out=u_sb[:, 0], in0=cells[:, 0], in1=cells[:, 1], op=ADD)
        nc.gpsimd.tensor_tensor(out=u_sb[:, 1], in0=cells[:, 0], in1=cells[:, 1], op=SUB)
        haar = const.tile([P, HALF_W // 2, 2, 2], BF16)
        columns = u_sb[:].rearrange("k v j q -> k q j v")
        nc.gpsimd.tensor_tensor(out=haar[:, :, 0, :], in0=columns[:, 0], in1=columns[:, 1], op=ADD)
        nc.gpsimd.tensor_tensor(out=haar[:, :, 1, :], in0=columns[:, 0], in1=columns[:, 1], op=SUB)

        w_words = w_sb[:].bitcast(F32).rearrange("o (c u) -> o u c", u=2)
        a_ps = psa.tile([P, BANK], F32)
        for u in range(2):
            nc.tensor.transpose(a_ps[:, u * O : (u + 1) * O], w_words[:, u, :], ident[:])
        w_grouped = const.tile([P, 4 * O], BF16, align_bytes=64)
        nc.scalar.copy(
            out=w_grouped[:].bitcast(F32).rearrange("c (o u) -> c o u", u=2),
            in_=a_ps[:, 0 : 2 * O].rearrange("c (u o) -> c o u", u=2),
        )
        w_codes = const.tile([P, O], U32, align_bytes=64)
        w_scales = const.tile([P, O], U8, align_bytes=64)

        def turn(k):
            for half in range(2):
                flip(("x", k, half), middle_rows(k, half), x_blocks_of(k, half), 2 * P)
            for half in range(2):
                flip_copy(spool_x, ("x", k, half), x_blocks_of(k, half))

        for k in range(NCH):
            if k + AHEAD < NCH:
                load(k + AHEAD)
            if k >= 1 and t_pairs(k - 1):
                haar_store(k - 1)
            if k >= 3:
                emit(k - 3)
            if 1 <= k < NCH - 2:
                for half in range(2):
                    flip(("x", k + 2, half), middle_rows(k + 2, half), x_blocks_of(k + 2, half), 2 * P)
            if t_pairs(k):
                haar_flip(k)
            if 1 <= k < NCH - 2:
                for half in range(2):
                    flip_copy(spool_x, ("x", k + 2, half), x_blocks_of(k + 2, half))
            if t_pairs(k):
                haar_copy(k)
            z_sb = zpool.tile([P, 3, NG, 2, RUN], F32)
            zt[k] = z_sb
            for half in range(2):
                if k == 0:
                    for r0, r1 in HEAD_ROWS:
                        if r0 // PAIRS == half:
                            rows = x_first[:, r0:r1, :].rearrange("p (i r) w -> p r i w", r=2)
                            for v, op in ((0, ADD), (1, SUB)):
                                vertical(0, rows[:, 0], rows[:, 1], r0 // 2 * PAIR_G, (r1 - r0) // 2, v, op)
                else:
                    vertical_half(k, half)
                if 1 <= k < NCH - 1:
                    flip_back(("x", k + 1, half), x_blocks_of(k + 1, half))
                if v_groups(k) > half * HG:
                    negate(k, half * HG, min(v_groups(k), half * HG + HG))
                if k == 0 and half == 0:
                    turn(1)
                    for h in range(2):
                        flip_back(("x", 1, h), x_blocks_of(1, h))
                if k >= 1:
                    ready = range(2 * half, min(2 * half + 2, parts(k)))
                    even_flips(k, ready)
                    if k == NCH - 1 and half == 0:
                        even_backs(k, ready)
            if t_pairs(k):
                haar_multiply(k)
            if k == 0:
                nc.vector.quantize_mx(out=w_codes[:].bitcast(FP8X4), scales=w_scales[:], in_=w_grouped[:])
            if k >= 2:
                for part in range(parts(k - 1)):
                    horizontal_psum(k - 1, part)
            if 1 <= k < NCH - 1:
                even_backs(k, range(parts(k)))
            if k >= 2:
                quantise(k - 2, 0, NP)
            if k == NCH - 1:
                quantise(k - 1, 0, NP)
            g_sb = gpool.tile([P, 4 * NP], BF16, align_bytes=64)
            gt[k] = g_sb
            if k == NCH - 1:
                haar_store(k)
                emit(k - 2, queue=nc.sync)
                even_backs(k, ready)
            if k == 0:
                horizontal_sbuf(nc.vector, 0, 0, v_groups(0))
            horizontal_gpsimd(k, v_groups(k), n_groups(k))
            if k == 0:
                turn(2)

        last = NCH - 1
        emit(last - 1, spare=True, queue=nc.sync)
        for part in range(parts(last)):
            horizontal_psum(last, part)
        for c0, by_vector in ((0, False), (N_TILE, True)):
            quantise(last, c0, c0 + N_TILE)
            multiply(last, c0, c0 + N_TILE, by_vector=by_vector)
            store(last, c0, c0 + N_TILE, nc.sync)
